import numpy as np
import ml_dtypes


def mxq(x, axis, fmt="e4m3"):
    dtype, down = {"e4m3": (ml_dtypes.float8_e4m3fn, 7), "e5m2": (ml_dtypes.float8_e5m2, 14)}[fmt]
    v = np.moveaxis(np.asarray(x, np.float32).astype(ml_dtypes.bfloat16).astype(np.float64), axis, -1)
    blocks = v.reshape(v.shape[:-1] + (-1, 32))
    amax = np.abs(blocks).max(-1, keepdims=True)
    byte = np.maximum(np.where(amax > 0, np.frexp(amax)[1] - 1 + 127, 0) - down, 1)
    scale = np.exp2(byte - 127.0)
    codes = (blocks / scale).astype(np.float32).astype(dtype).astype(np.float64)
    return np.moveaxis((codes * scale).reshape(v.shape), -1, axis)


WIDE = False


def mx_kscale(k):
    if not WIDE:
        return np.ones(k)
    levels = np.array([30, -30])
    if k % 512:
        return np.exp2(np.random.permutation(np.resize(levels, k // 32))).repeat(32)
    a = np.empty((k // 512, 16))
    for p in range(k // 512):
        a[p, :8] = np.random.permutation(np.resize(levels, 8))
        for g in range(8):
            far = levels[np.abs(levels - a[p, g]) >= 10]
            a[p, g + 8] = far[np.random.randint(len(far))]
    return np.exp2(a.ravel()).repeat(32)


BF16 = ml_dtypes.bfloat16


def bf(x):
    return np.asarray(x, np.float32).astype(BF16)


def f64(x):
    return np.asarray(x).astype(np.float64)


B, D, H, K = 5120, 1024, 1024, 128
EPS_B = 1e-8


def silu(v):
    return v / (1.0 + np.exp(-v))


def softplus(v):
    return np.maximum(v, 0.0) + np.log(1.0 + np.exp(-np.abs(v)))


def setup_inputs():
    s = mx_kscale(H)
    return {"h_act": bf(silu(np.random.standard_normal((B, H))) * s),
            "W3": bf(np.random.standard_normal((H, K)) * 3.0 / np.sqrt(H) / s[:, None]),
            "b3": bf(0.5 * np.random.standard_normal(K))}


def reference(h_act, W3, b3):
    logits = (mxq(f64(h_act), 1, "e5m2") @ mxq(f64(W3), 0, "e4m3")) + f64(b3)
    evidence = softplus(logits)
    alpha = evidence + 1.0
    S = alpha.sum(-1, keepdims=True)
    expected_prob = alpha / S
    vacuity = float(K) / S[:, 0]
    belief = evidence / S
    full = np.zeros(belief.shape[0])
    for i in range(K):
        bi = belief[:, i:i + 1]
        full = full + ((1.0 - np.abs(bi - belief) / (bi + belief + EPS_B)) * bi * belief).sum(-1)
    dissonance = 0.5 * (full - (belief * belief).sum(-1))
    return (alpha, evidence, expected_prob, vacuity, dissonance)

@@ -1,0 +1,389 @@
+import math
+from contextlib import ExitStack
+
+import concourse.mybir as mybir
+from concourse.masks import make_identity
+
+ROWS, H, K = 5120, 1024, 128
+EPS = 1e-8
+FLOPS = 2 * ROWS * H * K
+
+F32 = mybir.dt.float32
+BF16 = mybir.dt.bfloat16
+U32 = mybir.dt.uint32
+U8 = mybir.dt.uint8
+E5M2X4 = mybir.dt.float8_e5m2_x4
+E4M3X4 = mybir.dt.float8_e4m3fn_x4
+ACT = mybir.ActivationFunctionType
+ALU = mybir.AluOpType
+
+P = 128
+TILES = ROWS // P
+GT = 4
+GROUPS = TILES // GT
+STAGES = GROUPS // 2
+PASSES = H // 512
+DEGREE = 12
+BLOCK = 16
+BLOCKS = K // BLOCK
+BLOCK_COLS = BLOCK * TILES
+CHUNKS_PER_BLOCK = BLOCK_COLS // P
+CHUNKS = BLOCKS * CHUNKS_PER_BLOCK
+BANK_CHUNKS = 4
+DL_STEP = 4
+RECIP_STEP = 13
+PROD_LAG = 2
+
+
+def ratio_polynomial(degree):
+    rho = 3.0 - math.sqrt(8.0)
+    cheb = [[1.0], [-1.0, 2.0]]
+    for n in range(2, degree + 1):
+        nxt = [0.0] * (n + 1)
+        for i, v in enumerate(cheb[n - 1]):
+            nxt[i] -= 2.0 * v
+            nxt[i + 1] += 4.0 * v
+        for i, v in enumerate(cheb[n - 2]):
+            nxt[i] -= v
+        cheb.append(nxt)
+    coef = [0.0] * (degree + 1)
+    for n in range(degree + 1):
+        weight = 4.0 / math.sqrt(8.0) * (1.0 if n == 0 else 2.0) * (-rho) ** n
+        for i, v in enumerate(cheb[n]):
+            coef[i] += weight * v
+    coef[0] -= 1.0
+    return coef
+
+
+def tile_evidentialhead_pb_kernel(tc, h_act, W3, b3, out_0, out_1, out_2, out_3, out_4):
+    nc = tc.nc
+    coef = ratio_polynomial(DEGREE)
+    half_eps = EPS / 2
+    m_scale = math.sqrt(1.0 + coef[0])
+    m_bias = m_scale * EPS * coef[0] / (1.0 + coef[0]) / 2
+    pairs = K * (K - 1) // 2
+
+    h_rows = h_act.rearrange("(p t) k -> p t k", t=TILES)
+    alpha_rows = out_0.rearrange("(p t) c -> p t c", t=TILES)
+    evidence_rows = out_1.rearrange("(p t) c -> p t c", t=TILES)
+    prob_rows = out_2.rearrange("(p t) c -> p t c", t=TILES)
+    vacuity_rows = out_3.rearrange("(p t) -> p t", t=TILES)
+    dissonance_rows = out_4.rearrange("(p t) -> p t", t=TILES)
+
+    with ExitStack() as ctx:
+        keep = ctx.enter_context(tc.tile_pool(name="keep", bufs=1))
+        ring = ctx.enter_context(tc.tile_pool(name="ring", bufs=2))
+        psum = ctx.enter_context(tc.psum_pool(name="psum", bufs=1))
+        ctx.enter_context(tc.manual_schedule())
+
+        ident = keep.tile([P, P], F32)
+        w_raw = keep.tile([P, PASSES, 4, K], BF16)
+        w_grouped = keep.tile([P, PASSES * K * 4], BF16, align_bytes=64)
+        w_codes = keep.tile([P, PASSES * K], U32, align_bytes=64)
+        w_scales = keep.tile([P, PASSES * K], U8, align_bytes=64)
+        bias = keep.tile([P, 1], BF16)
+        ev_sum = keep.tile([P, TILES], F32)
+        strength = keep.tile([P, TILES], F32)
+        inv_s = keep.tile([P, TILES], F32)
+        vacuity = keep.tile([P, TILES], F32)
+        dissonance = keep.tile([P, TILES], F32)
+        sorted_all = keep.tile([P, K, TILES], F32)
+        log_step = keep.tile([P, K, TILES], F32)
+        pick = keep.tile([P, CHUNKS_PER_BLOCK, TILES], F32)
+        pick_rank = keep.tile([P, BLOCKS, CHUNKS_PER_BLOCK, TILES], F32)
+
+        h_sb, h_t, h_codes, h_scales = {}, {}, {}, {}
+        soft, relu, evidence, belief, sort_buf, log_u = {}, {}, {}, {}, {}, {}
+        power, g_bank, u_sq, m_sq = {}, {}, {}, {}
+
+        def tiles_of(g):
+            return slice(g * GT, (g + 1) * GT)
+
+        def load(g):
+            h_sb[g] = ring.tile([P, GT, H], BF16, name="h_sb")
+            nc.sync.dma_start(out=h_sb[g][:], in_=h_rows[:, tiles_of(g), :])
+
+        def transpose_h(g):
+            h_t[g] = ring.tile([P, PASSES * GT * P * 4], BF16, name="h_t", align_bytes=64)
+            words_out = h_t[g][:].bitcast(F32).rearrange("p (s t r u) -> p s t r u", s=PASSES, t=GT, u=2)
+            for t in range(GT):
+                words = h_sb[g][:, t, :].bitcast(F32)
+                bank = psum.tile([P, PASSES, 2, P], F32, name="wide", bufs=4)
+                for s in range(PASSES):
+                    for u in range(2):
+                        nc.tensor.transpose(bank[:, s, u, :], words[:, 256 * s + u : 256 * (s + 1) : 2], ident[:])
+                nc.scalar.copy(out=words_out[:, :, t, :, :], in_=bank[:].rearrange("p s u r -> p s r u"))
+
+        def quantize_h(g):
+            h_codes[g] = ring.tile([P, PASSES * GT * P], U32, name="h_codes", align_bytes=64)
+            h_scales[g] = ring.tile([P, PASSES * GT * P], U8, name="h_scales", align_bytes=64)
+            nc.vector.quantize_mx(out=h_codes[g][:].bitcast(E5M2X4), scales=h_scales[g][:], in_=h_t[g][:])
+
+        def logits(g):
+            acc = psum.tile([P, GT * P], F32, name="pair", bufs=2)
+            for s in range(PASSES):
+                w_cols = slice(s * K, (s + 1) * K)
+                h_cols = slice(s * GT * P, (s + 1) * GT * P)
+                nc.tensor.matmul_mx(
+                    out=acc[:],
+                    lhsT=w_codes[:, w_cols].bitcast(E4M3X4),
+                    lhsT_scale=w_scales[:, w_cols],
+                    rhs=h_codes[g][:, h_cols].bitcast(E5M2X4),
+                    rhs_scale=h_scales[g][:, h_cols],
+                    start=(s == 0),
+                    stop=(s == PASSES - 1),
+                )
+            soft[g] = ring.tile([P, GT * P], F32, name="soft")
+            relu[g] = ring.tile([P, GT * P], F32, name="relu")
+            nc.scalar.activation(out=soft[g][:], in_=acc[:], func=ACT.Abs, bias=bias[:])
+            nc.scalar.activation(out=relu[g][:], in_=acc[:], func=ACT.Relu, bias=bias[:])
+            nc.scalar.activation(out=soft[g][:], in_=soft[g][:], func=ACT.Exp, scale=-1.0)
+
+        def softplus_log(g):
+            nc.scalar.activation(out=soft[g][:], in_=soft[g][:], func=ACT.Ln, bias=1.0)
+
+        def evidence_rows_out(g):
+            bank = psum.tile([P, GT, K], F32, name="ev_bank")
+            evidence[g] = ring.tile([P, GT, K], F32, name="evidence")
+            for t in range(GT):
+                cols = slice(t * P, (t + 1) * P)
+                nc.tensor.matmul(bank[:, t, :], lhsT=relu[g][:, cols], rhs=ident[:], is_transpose=True, start=True, stop=False)
+                nc.tensor.matmul(bank[:, t, :], lhsT=soft[g][:, cols], rhs=ident[:], is_transpose=True, start=False, stop=True)
+            for t in range(GT):
+                col = g * GT + t
+                nc.scalar.activation(out=evidence[g][:, t, :], in_=bank[:, t, :], func=ACT.Identity, accum_out=ev_sum[:, col : col + 1])
+            nc.sync.dma_start(out=evidence_rows[:, tiles_of(g), :], in_=evidence[g][:])
+
+        def alpha_out(g):
+            alpha = ring.tile([P, GT, K], F32, name="alpha")
+            nc.scalar.activation(out=alpha[:], in_=evidence[g][:], func=ACT.Identity, bias=1.0)
+            nc.sync.dma_start(out=alpha_rows[:, tiles_of(g), :], in_=alpha[:])
+
+        def stage_cols(j):
+            return slice(2 * j * GT, 2 * (j + 1) * GT)
+
+        def add_classes(j):
+            nc.vector.tensor_scalar(out=strength[:, stage_cols(j)], in0=ev_sum[:, stage_cols(j)], scalar1=float(K), scalar2=None, op0=ALU.add)
+
+        def invert(j):
+            nc.vector.reciprocal(out=inv_s[:, stage_cols(j)], in_=strength[:, stage_cols(j)])
+
+        def belief_of(g):
+            belief[g] = ring.tile([P, GT, K], F32, name="belief", bufs=4)
+            for t in range(GT):
+                col = g * GT + t
+                nc.scalar.activation(out=belief[g][:, t, :], in_=evidence[g][:, t, :], func=ACT.Copy, scale=inv_s[:, col : col + 1])
+
+        def prob_out(g):
+            prob = ring.tile([P, GT, K], F32, name="prob")
+            for t in range(GT):
+                col = g * GT + t
+                nc.scalar.activation(out=prob[:, t, :], in_=evidence[g][:, t, :], func=ACT.Identity, scale=inv_s[:, col : col + 1], bias=inv_s[:, col : col + 1])
+            nc.sync.dma_start(out=prob_rows[:, tiles_of(g), :], in_=prob[:])
+
+        def exchange(dst, src):
+            nc.vector.tensor_tensor(out=dst[0], in0=src[0], in1=src[1], op=ALU.max)
+            nc.vector.tensor_tensor(out=dst[1], in0=src[0], in1=src[1], op=ALU.min)
+
+        def sort_step(g, number, p, k):
+            if number == 0:
+                first = ring.tile([P, K * GT], F32, name="sort_a", bufs=4)
+                second = ring.tile([P, K * GT], F32, name="sort_b", bufs=2)
+                sort_buf[g] = (second, first)
+                src = belief[g][:].rearrange("p t (two c) -> p two c t", two=2)
+                dst = second[:].rearrange("p (c two t) -> p two c t", two=2, t=GT)
+                exchange((dst[:, 0], dst[:, 1]), (src[:, 0], src[:, 1]))
+                return
+            src_buf, dst_buf = sort_buf[g][(number - 1) % 2], sort_buf[g][number % 2]
+            if k == p:
+                src = src_buf[:].rearrange("p (n two q) -> p two n q", two=2, q=p * GT)
+                dst = dst_buf[:].rearrange("p (n two q) -> p two n q", two=2, q=p * GT)
+                exchange((dst[:, 0], dst[:, 1]), (src[:, 0], src[:, 1]))
+                return
+            inner = slice(k * GT, (2 * p - k) * GT)
+            src = src_buf[:].rearrange("p (n w) -> p n w", w=2 * p * GT)[:, :, inner].rearrange("p n (g two q) -> p two n g q", two=2, q=k * GT)
+            dst = dst_buf[:].rearrange("p (n w) -> p n w", w=2 * p * GT)[:, :, inner].rearrange("p n (g two q) -> p two n g q", two=2, q=k * GT)
+            exchange((dst[:, 0], dst[:, 1]), (src[:, 0], src[:, 1]))
+
+        def copy_ends(g, number, p):
+            src_buf, dst_buf = sort_buf[g][number % 2], sort_buf[g][(number + 1) % 2]
+            src = src_buf[:].rearrange("p (n f q) -> p n f q", f=4, q=p * GT // 2)[:, :, 0:4:3, :]
+            dst = dst_buf[:].rearrange("p (n f q) -> p n f q", f=4, q=p * GT // 2)[:, :, 0:4:3, :]
+            nc.vector.tensor_copy(out=dst, in_=src)
+
+        steps = [(1 << a, 1 << b) for a in range(7) for b in range(a, -1, -1)]
+
+        def take_sorted(j):
+            log_u[j] = ring.tile([P, K, 2 * GT], F32, name="log_u", bufs=1)
+            for i in range(2):
+                g = 2 * j + i
+                done = sort_buf[g][(len(steps) - 1) % 2][:].rearrange("p (c t) -> p c t", t=GT)
+                nc.scalar.activation(out=log_u[j][:, :, i * GT : (i + 1) * GT], in_=done, func=ACT.Ln, bias=half_eps)
+            for i in range(2):
+                g = 2 * j + i
+                done = sort_buf[g][(len(steps) - 1) % 2][:].rearrange("p (c t) -> p c t", t=GT)
+                nc.scalar.copy(out=sorted_all[:, :, tiles_of(g)], in_=done)
+
+        def log_steps(j):
+            nc.vector.tensor_tensor(out=log_step[:, 1:, stage_cols(j)], in0=log_u[j][:, 1:, :], in1=log_u[j][:, : K - 1, :], op=ALU.subtract)
+
+        def front(j):
+            for g in (2 * j, 2 * j + 1):
+                logits(g)
+            for g in (2 * j, 2 * j + 1):
+                softplus_log(g)
+            for g in (2 * j, 2 * j + 1):
+                evidence_rows_out(g)
+            for g in (2 * j, 2 * j + 1):
+                alpha_out(g)
+
+        def scaled(j):
+            for g in (2 * j, 2 * j + 1):
+                belief_of(g)
+            for g in (2 * j, 2 * j + 1):
+                prob_out(g)
+
+        def build_picks():
+            over = keep.tile([P, CHUNKS_PER_BLOCK, BLOCK - 1], F32)
+            local = keep.tile([P, CHUNKS_PER_BLOCK], F32)
+            local_start = keep.tile([P, CHUNKS_PER_BLOCK], F32)
+            offset = keep.tile([P, CHUNKS_PER_BLOCK, TILES], F32)
+            rank = keep.tile([P, BLOCKS, CHUNKS_PER_BLOCK], F32)
+            nc.gpsimd.iota(over[:], [[P, CHUNKS_PER_BLOCK], [-TILES, BLOCK - 1]], base=-TILES, channel_multiplier=1, allow_small_or_imprecise_dtypes=True)
+            nc.gpsimd.iota(offset[:], [[P, CHUNKS_PER_BLOCK], [-1, TILES]], base=0, channel_multiplier=1, allow_small_or_imprecise_dtypes=True)
+            nc.gpsimd.iota(rank[:], [[BLOCK, BLOCKS], [0, CHUNKS_PER_BLOCK]], base=0, channel_multiplier=0, allow_small_or_imprecise_dtypes=True)
+            nc.vector.tensor_scalar(out=over[:], in0=over[:], scalar1=0.0, scalar2=None, op0=ALU.is_ge)
+            nc.vector.tensor_reduce(out=local[:], in_=over[:], axis=mybir.AxisListType.X, op=ALU.add)
+            nc.vector.tensor_scalar(out=local_start[:], in0=local[:], scalar1=float(TILES), scalar2=None, op0=ALU.mult)
+            nc.vector.tensor_tensor(out=rank[:], in0=rank[:], in1=local[:].unsqueeze(1).to_broadcast([P, BLOCKS, CHUNKS_PER_BLOCK]), op=ALU.add)
+            nc.vector.tensor_tensor(out=pick[:], in0=offset[:], in1=local_start[:].unsqueeze(2).to_broadcast([P, CHUNKS_PER_BLOCK, TILES]), op=ALU.is_equal)
+            shape = [P, BLOCKS, CHUNKS_PER_BLOCK, TILES]
+            nc.vector.tensor_tensor(out=pick_rank[:], in0=pick[:].unsqueeze(1).to_broadcast(shape), in1=rank[:].unsqueeze(3).to_broadcast(shape), op=ALU.mult)
+
+        make_identity(nc, ident[:])
+        load(0)
+        nc.sync.dma_start(out=w_raw[:], in_=W3.rearrange("(s p j) n -> p s j n", s=PASSES, j=4))
+        nc.sync.dma_start(out=bias[:], in_=b3.rearrange("(p o) -> p o", o=1))
+        load(1)
+        build_picks()
+        nc.vector.tensor_copy(out=w_grouped[:].rearrange("p (s n j) -> p s n j", s=PASSES, j=4), in_=w_raw[:].rearrange("p s j n -> p s n j"))
+        transpose_h(0)
+        load(2)
+        transpose_h(1)
+        load(3)
+        nc.vector.quantize_mx(out=w_codes[:].bitcast(E4M3X4), scales=w_scales[:], in_=w_grouped[:])
+        quantize_h(0)
+        quantize_h(1)
+        front(0)
+        add_classes(0)
+        invert(0)
+        scaled(0)
+        transpose_h(2)
+        transpose_h(3)
+
+        for j in range(STAGES):
+            if j + 2 < STAGES:
+                load(2 * j + 4)
+                load(2 * j + 5)
+            if j + 1 < STAGES:
+                quantize_h(2 * j + 2)
+                quantize_h(2 * j + 3)
+            if j > 0:
+                take_sorted(j - 1)
+            if j + 1 < STAGES:
+                front(j + 1)
+            for number, (p, k) in enumerate(steps):
+                for g in (2 * j, 2 * j + 1):
+                    sort_step(g, number, p, k)
+                if k == p and p > 1:
+                    for g in (2 * j, 2 * j + 1):
+                        copy_ends(g, number, p)
+                if number == DL_STEP and j > 0:
+                    log_steps(j - 1)
+                if number == RECIP_STEP and j + 1 < STAGES:
+                    add_classes(j + 1)
+                if number == RECIP_STEP + 1 and j + 1 < STAGES:
+                    invert(j + 1)
+                    scaled(j + 1)
+                    if j + 2 < STAGES:
+                        transpose_h(2 * j + 4)
+                        transpose_h(2 * j + 5)
+        take_sorted(STAGES - 1)
+        nc.vector.tensor_scalar(out=vacuity[:], in0=inv_s[:], scalar1=float(K), scalar2=None, op0=ALU.mult)
+        nc.sync.dma_start(out=vacuity_rows, in_=vacuity[:])
+        log_steps(STAGES - 1)
+
+        total = psum.tile([P, TILES], F32, name="total")
+        sorted_flat = sorted_all[:].rearrange("p c t -> p (c t)")
+        log_flat = log_step[:].rearrange("p c t -> p (c t)")
+
+        def powers(b):
+            skip = TILES if b == 0 else 0
+            for n in range(1, DEGREE + 1):
+                power[b, n] = ring.tile([P, BLOCK_COLS], F32, name="power%d" % n)
+                if b == 0:
+                    nc.gpsimd.memset(power[b, n][:, :TILES], 0.0)
+                nc.scalar.activation(out=power[b, n][:, skip:], in_=log_flat[:, b * BLOCK_COLS + skip : (b + 1) * BLOCK_COLS], func=ACT.Exp, scale=float(n))
+
+        def squares(e):
+            bank = psum.tile([P, BANK_CHUNKS, P], F32, name="pair", bufs=2)
+            for i in range(BANK_CHUNKS):
+                c = e * BANK_CHUNKS + i
+                nc.tensor.transpose(bank[:, i, :], sorted_flat[:, c * P : (c + 1) * P], ident[:])
+            u_sq[e] = ring.tile([P, BANK_CHUNKS, P], F32, name="u_sq", bufs=3)
+            m_sq[e] = ring.tile([P, BANK_CHUNKS, P], F32, name="m_sq", bufs=3)
+            nc.scalar.activation(out=u_sq[e][:], in_=bank[:], func=ACT.Square, bias=half_eps)
+            nc.scalar.activation(out=m_sq[e][:], in_=bank[:], func=ACT.Square, scale=m_scale, bias=m_bias)
+
+        def recur(pos):
+            b, i = divmod(pos, BLOCK)
+            pb, pi = divmod(pos - 1, BLOCK)
+            for n in range(1, DEGREE + 1):
+                here = power[b, n][:, i * TILES : (i + 1) * TILES]
+                nc.vector.scalar_tensor_tensor(out=here, in0=power[pb, n][:, pi * TILES : (pi + 1) * TILES], scalar=coef[n], in1=here, op0=ALU.add, op1=ALU.mult)
+
+        def sum_powers(c):
+            e, i = divmod(c, BANK_CHUNKS)
+            b, j = divmod(c, CHUNKS_PER_BLOCK)
+            if i == 0:
+                g_bank[e] = psum.tile([P, BANK_CHUNKS, P], F32, name="wide", bufs=4)
+            for n in range(1, DEGREE + 1):
+                nc.tensor.matmul(g_bank[e][:, i, :], lhsT=power[b, n][:, j * P : (j + 1) * P], rhs=ident[:], is_transpose=True, start=(n == 1), stop=(n == DEGREE))
+
+        def weigh(e):
+            prod = ring.tile([P, BANK_CHUNKS, P], F32, name="prod")
+            nc.vector.scalar_tensor_tensor(
+                out=prod[:].rearrange("p i r -> p (i r)"), in0=u_sq[e][:].rearrange("p i r -> p (i r)"), scalar=-half_eps * half_eps,
+                in1=g_bank[e][:].rearrange("p i r -> p (i r)"), op0=ALU.add, op1=ALU.mult)
+            for i in range(BANK_CHUNKS):
+                c = e * BANK_CHUNKS + i
+                b, j = divmod(c, CHUNKS_PER_BLOCK)
+                nc.tensor.matmul(total[:], lhsT=m_sq[e][:, i, :], rhs=pick_rank[:, b, j, :], start=(c == 0), stop=False)
+                nc.tensor.matmul(total[:], lhsT=prod[:, i, :], rhs=pick[:, j, :], start=False, stop=(c == CHUNKS - 1))
+
+        def last_pos(c):
+            return ((c + 1) * P - 1) // TILES
+
+        banks = CHUNKS // BANK_CHUNKS
+        bank_done = [last_pos((e + 1) * BANK_CHUNKS - 1) for e in range(banks)]
+
+        def feed(b):
+            powers(b)
+            for e in range(banks):
+                if bank_done[e] // BLOCK == b:
+                    squares(e)
+
+        feed(0)
+        feed(1)
+        for pos in range(1, K):
+            recur(pos)
+            if pos % BLOCK == 0 and pos // BLOCK + 1 < BLOCKS:
+                feed(pos // BLOCK + 1)
+            for c in range(CHUNKS):
+                if last_pos(c) == pos:
+                    sum_powers(c)
+            for e in range(banks):
+                if min(bank_done[e] + PROD_LAG, K - 1) == pos:
+                    weigh(e)
+        nc.vector.tensor_scalar(out=dissonance[:], in0=total[:], scalar1=-m_bias * m_bias * pairs, scalar2=None, op0=ALU.add)
+        nc.sync.dma_start(out=dissonance_rows, in_=dissonance[:])

@@ -26,13 +26,13 @@ PASSES = H // 512
 DEGREE = 12
 BLOCK = 16
 BLOCKS = K // BLOCK
-BLOCK_COLS = BLOCK * TILES
-CHUNKS_PER_BLOCK = BLOCK_COLS // P
-CHUNKS = BLOCKS * CHUNKS_PER_BLOCK
+GROUP_COLS = BLOCK * GT
+BLOCK_COLS = GROUPS * GROUP_COLS
 BANK_CHUNKS = 4
+FIRST_BANK = 3
+ABOVE_ALL = 128.0
 DL_STEP = 4
 RECIP_STEP = 13
-PROD_LAG = 2
 
 
 def ratio_polynomial(degree):
@@ -87,32 +87,39 @@ def tile_evidentialhead_pb_kernel(tc, h_act, W3, b3, out_0, out_1, out_2, out_3,
         inv_s = keep.tile([P, TILES], F32)
         vacuity = keep.tile([P, TILES], F32)
         dissonance = keep.tile([P, TILES], F32)
-        sorted_all = keep.tile([P, K, TILES], F32)
-        log_step = keep.tile([P, K, TILES], F32)
-        pick = keep.tile([P, CHUNKS_PER_BLOCK, TILES], F32)
-        pick_rank = keep.tile([P, BLOCKS, CHUNKS_PER_BLOCK, TILES], F32)
+        u_sq = keep.tile([P, BLOCKS, STAGES, P], F32)
+        log_step = keep.tile([P, BLOCKS, GROUPS, GROUP_COLS], F32)
+        log_u = keep.tile([P, 2, GT + K * GT], F32)
+        pick = keep.tile([P, 2 * GT], F32)
+        pick_rank = keep.tile([P, BLOCKS, 2 * GT], F32)
+        total = psum.tile([P, TILES], F32, name="total")
 
         h_sb, h_t, h_codes, h_scales = {}, {}, {}, {}
-        soft, relu, evidence, belief, sort_buf, log_u = {}, {}, {}, {}, {}, {}
-        power, g_bank, u_sq, m_sq = {}, {}, {}, {}
+        soft, relu, evidence, belief, sort_buf, by_block = {}, {}, {}, {}, {}, {}
+        power, g_bank, m_sq = {}, {}, {}
 
         def tiles_of(g):
             return slice(g * GT, (g + 1) * GT)
 
-        def load(g):
-            h_sb[g] = ring.tile([P, GT, H], BF16, name="h_sb")
-            nc.sync.dma_start(out=h_sb[g][:], in_=h_rows[:, tiles_of(g), :])
+        def load(g, first=0, count=GT):
+            if first == 0:
+                h_sb[g] = ring.tile([P, GT, H], BF16, name="h_sb")
+            nc.sync.dma_start(out=h_sb[g][:, first : first + count, :], in_=h_rows[:, g * GT + first : g * GT + first + count, :])
 
-        def transpose_h(g):
-            h_t[g] = ring.tile([P, PASSES * GT * P * 4], BF16, name="h_t", align_bytes=64)
+        def transpose_h(g, which=range(GT), on_vector=()):
+            if which[0] == 0:
+                h_t[g] = ring.tile([P, PASSES * GT * P * 4], BF16, name="h_t", align_bytes=64)
             words_out = h_t[g][:].bitcast(F32).rearrange("p (s t r u) -> p s t r u", s=PASSES, t=GT, u=2)
-            for t in range(GT):
+            for t in which:
                 words = h_sb[g][:, t, :].bitcast(F32)
                 bank = psum.tile([P, PASSES, 2, P], F32, name="wide", bufs=4)
                 for s in range(PASSES):
                     for u in range(2):
                         nc.tensor.transpose(bank[:, s, u, :], words[:, 256 * s + u : 256 * (s + 1) : 2], ident[:])
-                nc.scalar.copy(out=words_out[:, :, t, :, :], in_=bank[:].rearrange("p s u r -> p s r u"))
+                if t in on_vector:
+                    nc.vector.tensor_copy(out=words_out[:, :, t, :, :], in_=bank[:].rearrange("p s u r -> p s r u"))
+                else:
+                    nc.scalar.copy(out=words_out[:, :, t, :, :], in_=bank[:].rearrange("p s u r -> p s r u"))
 
         def quantize_h(g):
             h_codes[g] = ring.tile([P, PASSES * GT * P], U32, name="h_codes", align_bytes=64)
@@ -162,11 +169,15 @@ def tile_evidentialhead_pb_kernel(tc, h_act, W3, b3, out_0, out_1, out_2, out_3,
         def stage_cols(j):
             return slice(2 * j * GT, 2 * (j + 1) * GT)
 
-        def add_classes(j):
-            nc.vector.tensor_scalar(out=strength[:, stage_cols(j)], in0=ev_sum[:, stage_cols(j)], scalar1=float(K), scalar2=None, op0=ALU.add)
+        def add_classes(cols):
+            nc.vector.tensor_scalar(out=strength[:, cols], in0=ev_sum[:, cols], scalar1=float(K), scalar2=None, op0=ALU.add)
 
-        def invert(j):
-            nc.vector.reciprocal(out=inv_s[:, stage_cols(j)], in_=strength[:, stage_cols(j)])
+        def invert(cols):
+            nc.vector.reciprocal(out=inv_s[:, cols], in_=strength[:, cols])
+
+        def belief_on_vector(g):
+            belief[g] = ring.tile([P, GT, K], F32, name="belief", bufs=4)
+            nc.vector.tensor_tensor(out=belief[g][:], in0=evidence[g][:], in1=inv_s[:, tiles_of(g)].unsqueeze(2).to_broadcast([P, GT, K]), op=ALU.mult)
 
         def belief_of(g):
             belief[g] = ring.tile([P, GT, K], F32, name="belief", bufs=4)
@@ -213,23 +224,45 @@ def tile_evidentialhead_pb_kernel(tc, h_act, W3, b3, out_0, out_1, out_2, out_3,
 
         steps = [(1 << a, 1 << b) for a in range(7) for b in range(a, -1, -1)]
 
-        def take_sorted(j):
-            log_u[j] = ring.tile([P, K, 2 * GT], F32, name="log_u", bufs=1)
-            for i in range(2):
-                g = 2 * j + i
-                done = sort_buf[g][(len(steps) - 1) % 2][:].rearrange("p (c t) -> p c t", t=GT)
-                nc.scalar.activation(out=log_u[j][:, :, i * GT : (i + 1) * GT], in_=done, func=ACT.Ln, bias=half_eps)
-            for i in range(2):
-                g = 2 * j + i
-                done = sort_buf[g][(len(steps) - 1) % 2][:].rearrange("p (c t) -> p c t", t=GT)
-                nc.scalar.copy(out=sorted_all[:, :, tiles_of(g)], in_=done)
+        def sorted_of(g):
+            return sort_buf[g][(len(steps) - 1) % 2]
 
-        def log_steps(j):
-            nc.vector.tensor_tensor(out=log_step[:, 1:, stage_cols(j)], in0=log_u[j][:, 1:, :], in1=log_u[j][:, : K - 1, :], op=ALU.subtract)
+        def take_logs(j):
+            for i in range(2):
+                nc.scalar.activation(out=log_u[:, i, GT:], in_=sorted_of(2 * j + i)[:], func=ACT.Ln, bias=half_eps)
 
-        def front(j):
-            for g in (2 * j, 2 * j + 1):
-                logits(g)
+        def regroup(j):
+            by_block[j] = ring.tile([P, BLOCKS, 2, GROUP_COLS], F32, name="by_block", bufs=1)
+            for i in range(2):
+                nc.scalar.copy(out=by_block[j][:, :, i, :], in_=sorted_of(2 * j + i)[:].rearrange("p (b x) -> p b x", x=GROUP_COLS))
+
+        def log_steps(j, first, last):
+            cols = slice(first * GROUP_COLS, last * GROUP_COLS)
+            below = log_u[:, :, GT:][:, :, cols].rearrange("p i (b x) -> p b i x", x=GROUP_COLS)
+            above = log_u[:, :, : K * GT][:, :, cols].rearrange("p i (b x) -> p b i x", x=GROUP_COLS)
+            nc.vector.tensor_tensor(out=log_step[:, first:last, 2 * j : 2 * j + 2, :], in0=below, in1=above, op=ALU.subtract)
+
+        def squares(j):
+            m_sq[j] = ring.tile([P, BLOCKS, P], F32, name="m_sq", bufs=1)
+            for first in range(0, BLOCKS, BANK_CHUNKS):
+                bank = psum.tile([P, BANK_CHUNKS, P], F32, name="pair", bufs=2)
+                for i in range(BANK_CHUNKS):
+                    nc.tensor.transpose(bank[:, i, :], by_block[j][:, first + i, :, :].rearrange("p i x -> p (i x)"), ident[:])
+                nc.scalar.activation(out=u_sq[:, first : first + BANK_CHUNKS, j, :], in_=bank[:], func=ACT.Square, bias=half_eps)
+                nc.scalar.activation(out=m_sq[j][:, first : first + BANK_CHUNKS, :], in_=bank[:], func=ACT.Square, scale=m_scale, bias=m_bias)
+
+        def rank_terms(j):
+            for b in range(BLOCKS):
+                nc.tensor.matmul(total[:, stage_cols(j)], lhsT=m_sq[j][:, b, :], rhs=pick_rank[:, b, :], start=(j == 0 and b == 0), stop=False)
+
+        def powers(b, first, last, exponents):
+            cols = slice(first * GROUP_COLS, last * GROUP_COLS)
+            for n in exponents:
+                if first == 0:
+                    power[b, n] = ring.tile([P, BLOCK_COLS], F32, name="power%d" % n)
+                nc.scalar.activation(out=power[b, n][:, cols], in_=log_step[:, b, first:last, :].rearrange("p g x -> p (g x)"), func=ACT.Exp, scale=float(n))
+
+        def after_logits(j):
             for g in (2 * j, 2 * j + 1):
                 softplus_log(g)
             for g in (2 * j, 2 * j + 1):
@@ -244,43 +277,53 @@ def tile_evidentialhead_pb_kernel(tc, h_act, W3, b3, out_0, out_1, out_2, out_3,
                 prob_out(g)
 
         def build_picks():
-            over = keep.tile([P, CHUNKS_PER_BLOCK, BLOCK - 1], F32)
-            local = keep.tile([P, CHUNKS_PER_BLOCK], F32)
-            local_start = keep.tile([P, CHUNKS_PER_BLOCK], F32)
-            offset = keep.tile([P, CHUNKS_PER_BLOCK, TILES], F32)
-            rank = keep.tile([P, BLOCKS, CHUNKS_PER_BLOCK], F32)
-            nc.gpsimd.iota(over[:], [[P, CHUNKS_PER_BLOCK], [-TILES, BLOCK - 1]], base=-TILES, channel_multiplier=1, allow_small_or_imprecise_dtypes=True)
-            nc.gpsimd.iota(offset[:], [[P, CHUNKS_PER_BLOCK], [-1, TILES]], base=0, channel_multiplier=1, allow_small_or_imprecise_dtypes=True)
-            nc.gpsimd.iota(rank[:], [[BLOCK, BLOCKS], [0, CHUNKS_PER_BLOCK]], base=0, channel_multiplier=0, allow_small_or_imprecise_dtypes=True)
-            nc.vector.tensor_scalar(out=over[:], in0=over[:], scalar1=0.0, scalar2=None, op0=ALU.is_ge)
-            nc.vector.tensor_reduce(out=local[:], in_=over[:], axis=mybir.AxisListType.X, op=ALU.add)
-            nc.vector.tensor_scalar(out=local_start[:], in0=local[:], scalar1=float(TILES), scalar2=None, op0=ALU.mult)
-            nc.vector.tensor_tensor(out=rank[:], in0=rank[:], in1=local[:].unsqueeze(1).to_broadcast([P, BLOCKS, CHUNKS_PER_BLOCK]), op=ALU.add)
-            nc.vector.tensor_tensor(out=pick[:], in0=offset[:], in1=local_start[:].unsqueeze(2).to_broadcast([P, CHUNKS_PER_BLOCK, TILES]), op=ALU.is_equal)
-            shape = [P, BLOCKS, CHUNKS_PER_BLOCK, TILES]
-            nc.vector.tensor_tensor(out=pick_rank[:], in0=pick[:].unsqueeze(1).to_broadcast(shape), in1=rank[:].unsqueeze(3).to_broadcast(shape), op=ALU.mult)
+            place = keep.tile([P, P], F32)
+            local = keep.tile([P, 1], F32)
+            rank = keep.tile([P, BLOCKS], F32)
+            nc.gpsimd.iota(place[:], [[0, 2], [1, BLOCK], [0, GT]], base=0, channel_multiplier=0, allow_small_or_imprecise_dtypes=True)
+            nc.gpsimd.iota(rank[:], [[BLOCK, BLOCKS]], base=0, channel_multiplier=0, allow_small_or_imprecise_dtypes=True)
+            nc.vector.tensor_tensor(out=place[:], in0=place[:], in1=ident[:], op=ALU.mult)
+            nc.vector.tensor_reduce(out=pick[:].rearrange("p (i t) -> p i t", t=GT), in_=ident[:].rearrange("p (i c t) -> p i t c", i=2, t=GT), axis=mybir.AxisListType.X, op=ALU.add)
+            nc.vector.tensor_reduce(out=local[:], in_=place[:], axis=mybir.AxisListType.X, op=ALU.add)
+            nc.vector.tensor_scalar(out=rank[:], in0=rank[:], scalar1=local[:], scalar2=None, op0=ALU.add)
+            shape = [P, BLOCKS, 2 * GT]
+            nc.vector.tensor_tensor(out=pick_rank[:], in0=pick[:].unsqueeze(1).to_broadcast(shape), in1=rank[:].unsqueeze(2).to_broadcast(shape), op=ALU.mult)
 
         make_identity(nc, ident[:])
-        load(0)
+        nc.gpsimd.memset(log_u[:, :, :GT], ABOVE_ALL)
+        load(0, 0, 1)
         nc.sync.dma_start(out=w_raw[:], in_=W3.rearrange("(s p j) n -> p s j n", s=PASSES, j=4))
         nc.sync.dma_start(out=bias[:], in_=b3.rearrange("(p o) -> p o", o=1))
-        load(1)
+        for t in range(1, GT):
+            load(0, t, 1)
+        load(1, 0, 2)
+        load(1, 2, 2)
         build_picks()
         nc.vector.tensor_copy(out=w_grouped[:].rearrange("p (s n j) -> p s n j", s=PASSES, j=4), in_=w_raw[:].rearrange("p s j n -> p s n j"))
-        transpose_h(0)
-        load(2)
-        transpose_h(1)
-        load(3)
+        transpose_h(0, range(2), on_vector=(1,))
         nc.vector.quantize_mx(out=w_codes[:].bitcast(E4M3X4), scales=w_scales[:], in_=w_grouped[:])
+        transpose_h(0, range(2, GT), on_vector=(3,))
+        load(2)
+        transpose_h(1, range(1))
         quantize_h(0)
+        transpose_h(1, range(1, 2), on_vector=(1,))
+        logits(0)
+        transpose_h(1, range(2, GT), on_vector=(2, 3))
+        load(3)
         quantize_h(1)
-        front(0)
-        add_classes(0)
-        invert(0)
-        scaled(0)
+        logits(1)
+        after_logits(0)
+        for g in range(2):
+            add_classes(tiles_of(g))
+            invert(tiles_of(g))
+            belief_on_vector(g)
+        for g in range(2):
+            prob_out(g)
         transpose_h(2)
         transpose_h(3)
 
+        all_powers = range(1, DEGREE + 1)
+        halves = (all_powers[: DEGREE // 2], all_powers[DEGREE // 2 :])
         for j in range(STAGES):
             if j + 2 < STAGES:
                 load(2 * j + 4)
@@ -289,9 +332,14 @@ def tile_evidentialhead_pb_kernel(tc, h_act, W3, b3, out_0, out_1, out_2, out_3,
                 quantize_h(2 * j + 2)
                 quantize_h(2 * j + 3)
             if j > 0:
-                take_sorted(j - 1)
+                take_logs(j - 1)
+                regroup(j - 1)
             if j + 1 < STAGES:
-                front(j + 1)
+                logits(2 * j + 2)
+                logits(2 * j + 3)
+                after_logits(j + 1)
+            if j > 0:
+                squares(j - 1)
             for number, (p, k) in enumerate(steps):
                 for g in (2 * j, 2 * j + 1):
                     sort_step(g, number, p, k)
@@ -299,91 +347,72 @@ def tile_evidentialhead_pb_kernel(tc, h_act, W3, b3, out_0, out_1, out_2, out_3,
                     for g in (2 * j, 2 * j + 1):
                         copy_ends(g, number, p)
                 if number == DL_STEP and j > 0:
-                    log_steps(j - 1)
+                    log_steps(j - 1, 0, BLOCKS)
+                    if j + 1 == STAGES:
+                        for b in range(2):
+                            powers(b, 0, GROUPS - 2, all_powers)
                 if number == RECIP_STEP and j + 1 < STAGES:
-                    add_classes(j + 1)
+                    add_classes(stage_cols(j + 1))
                 if number == RECIP_STEP + 1 and j + 1 < STAGES:
-                    invert(j + 1)
+                    invert(stage_cols(j + 1))
                     scaled(j + 1)
                     if j + 2 < STAGES:
                         transpose_h(2 * j + 4)
                         transpose_h(2 * j + 5)
-        take_sorted(STAGES - 1)
+            if j > 0:
+                rank_terms(j - 1)
+        last = STAGES - 1
+        take_logs(last)
+        log_steps(last, 0, 2)
+        log_steps(last, 2, BLOCKS)
         nc.vector.tensor_scalar(out=vacuity[:], in0=inv_s[:], scalar1=float(K), scalar2=None, op0=ALU.mult)
         nc.sync.dma_start(out=vacuity_rows, in_=vacuity[:])
-        log_steps(STAGES - 1)
+        powers(0, GROUPS - 2, GROUPS, all_powers)
+        regroup(last)
+        powers(1, GROUPS - 2, GROUPS, all_powers)
+        squares(last)
+        rank_terms(last)
 
-        total = psum.tile([P, TILES], F32, name="total")
-        sorted_flat = sorted_all[:].rearrange("p c t -> p (c t)")
-        log_flat = log_step[:].rearrange("p c t -> p (c t)")
+        def at(b, n, i):
+            return power[b, n][:].rearrange("p (g c t) -> p g c t", c=BLOCK, t=GT)[:, :, i, :]
 
-        def powers(b):
-            skip = TILES if b == 0 else 0
-            for n in range(1, DEGREE + 1):
-                power[b, n] = ring.tile([P, BLOCK_COLS], F32, name="power%d" % n)
-                if b == 0:
-                    nc.gpsimd.memset(power[b, n][:, :TILES], 0.0)
-                nc.scalar.activation(out=power[b, n][:, skip:], in_=log_flat[:, b * BLOCK_COLS + skip : (b + 1) * BLOCK_COLS], func=ACT.Exp, scale=float(n))
+        def recur(b, exponents):
+            for i in range(BLOCK):
+                if b == 0 and i == 0:
+                    continue
+                pb, pi = divmod(b * BLOCK + i - 1, BLOCK)
+                for n in exponents:
+                    nc.vector.scalar_tensor_tensor(out=at(b, n, i), in0=at(pb, n, pi), scalar=coef[n], in1=at(b, n, i), op0=ALU.add, op1=ALU.mult)
 
-        def squares(e):
-            bank = psum.tile([P, BANK_CHUNKS, P], F32, name="pair", bufs=2)
-            for i in range(BANK_CHUNKS):
-                c = e * BANK_CHUNKS + i
-                nc.tensor.transpose(bank[:, i, :], sorted_flat[:, c * P : (c + 1) * P], ident[:])
-            u_sq[e] = ring.tile([P, BANK_CHUNKS, P], F32, name="u_sq", bufs=3)
-            m_sq[e] = ring.tile([P, BANK_CHUNKS, P], F32, name="m_sq", bufs=3)
-            nc.scalar.activation(out=u_sq[e][:], in_=bank[:], func=ACT.Square, bias=half_eps)
-            nc.scalar.activation(out=m_sq[e][:], in_=bank[:], func=ACT.Square, scale=m_scale, bias=m_bias)
+        bank_stages = (range(FIRST_BANK), range(FIRST_BANK, STAGES))
 
-        def recur(pos):
-            b, i = divmod(pos, BLOCK)
-            pb, pi = divmod(pos - 1, BLOCK)
-            for n in range(1, DEGREE + 1):
-                here = power[b, n][:, i * TILES : (i + 1) * TILES]
-                nc.vector.scalar_tensor_tensor(out=here, in0=power[pb, n][:, pi * TILES : (pi + 1) * TILES], scalar=coef[n], in1=here, op0=ALU.add, op1=ALU.mult)
+        def sum_powers(b, exponents):
+            for n in exponents:
+                for side, members in enumerate(bank_stages):
+                    if n == 1:
+                        g_bank[b, side] = psum.tile([P, len(members), P], F32, name="wide", bufs=4)
+                    for j in members:
+                        nc.tensor.matmul(
+                            g_bank[b, side][:, j - members[0], :], lhsT=power[b, n][:, j * P : (j + 1) * P], rhs=ident[:], is_transpose=True,
+                            start=(n == 1 and j == members[0]), stop=(n == DEGREE and j == members[-1]))
 
-        def sum_powers(c):
-            e, i = divmod(c, BANK_CHUNKS)
-            b, j = divmod(c, CHUNKS_PER_BLOCK)
-            if i == 0:
-                g_bank[e] = psum.tile([P, BANK_CHUNKS, P], F32, name="wide", bufs=4)
-            for n in range(1, DEGREE + 1):
-                nc.tensor.matmul(g_bank[e][:, i, :], lhsT=power[b, n][:, j * P : (j + 1) * P], rhs=ident[:], is_transpose=True, start=(n == 1), stop=(n == DEGREE))
+        def weigh(b):
+            for side, members in enumerate(bank_stages):
+                prod = ring.tile([P, len(members), P], F32, name="prod")
+                nc.vector.scalar_tensor_tensor(
+                    out=prod[:].rearrange("p i r -> p (i r)"), in0=u_sq[:, b, members[0] : members[-1] + 1, :].rearrange("p i r -> p (i r)"), scalar=-half_eps * half_eps,
+                    in1=g_bank[b, side][:].rearrange("p i r -> p (i r)"), op0=ALU.add, op1=ALU.mult)
+                for j in members:
+                    nc.tensor.matmul(total[:, stage_cols(j)], lhsT=prod[:, j - members[0], :], rhs=pick[:], start=False, stop=(b == BLOCKS - 1 and j == last))
 
-        def weigh(e):
-            prod = ring.tile([P, BANK_CHUNKS, P], F32, name="prod")
-            nc.vector.scalar_tensor_tensor(
-                out=prod[:].rearrange("p i r -> p (i r)"), in0=u_sq[e][:].rearrange("p i r -> p (i r)"), scalar=-half_eps * half_eps,
-                in1=g_bank[e][:].rearrange("p i r -> p (i r)"), op0=ALU.add, op1=ALU.mult)
-            for i in range(BANK_CHUNKS):
-                c = e * BANK_CHUNKS + i
-                b, j = divmod(c, CHUNKS_PER_BLOCK)
-                nc.tensor.matmul(total[:], lhsT=m_sq[e][:, i, :], rhs=pick_rank[:, b, j, :], start=(c == 0), stop=False)
-                nc.tensor.matmul(total[:], lhsT=prod[:, i, :], rhs=pick[:, j, :], start=False, stop=(c == CHUNKS - 1))
-
-        def last_pos(c):
-            return ((c + 1) * P - 1) // TILES
-
-        banks = CHUNKS // BANK_CHUNKS
-        bank_done = [last_pos((e + 1) * BANK_CHUNKS - 1) for e in range(banks)]
-
-        def feed(b):
-            powers(b)
-            for e in range(banks):
-                if bank_done[e] // BLOCK == b:
-                    squares(e)
-
-        feed(0)
-        feed(1)
-        for pos in range(1, K):
-            recur(pos)
-            if pos % BLOCK == 0 and pos // BLOCK + 1 < BLOCKS:
-                feed(pos // BLOCK + 1)
-            for c in range(CHUNKS):
-                if last_pos(c) == pos:
-                    sum_powers(c)
-            for e in range(banks):
-                if min(bank_done[e] + PROD_LAG, K - 1) == pos:
-                    weigh(e)
+        for b in range(BLOCKS):
+            for side, exponents in enumerate(halves):
+                recur(b, exponents)
+                if side == 0 and b > 0:
+                    weigh(b - 1)
+                sum_powers(b, exponents)
+                if 1 <= b < BLOCKS - 1:
+                    powers(b + 1, 0, GROUPS, exponents)
+        weigh(BLOCKS - 1)
         nc.vector.tensor_scalar(out=dissonance[:], in0=total[:], scalar1=-m_bias * m_bias * pairs, scalar2=None, op0=ALU.add)
         nc.sync.dma_start(out=dissonance_rows, in_=dissonance[:])

@@ -30,9 +30,10 @@ GROUP_COLS = BLOCK * GT
 BLOCK_COLS = GROUPS * GROUP_COLS
 BANK_CHUNKS = 4
 FIRST_BANK = 3
+JOINT = 6
+LANES = DEGREE - JOINT
+SLOTS = 3
 ABOVE_ALL = 128.0
-DL_STEP = 4
-RECIP_STEP = 13
 
 
 def ratio_polynomial(degree):
@@ -73,6 +74,7 @@ def tile_evidentialhead_pb_kernel(tc, h_act, W3, b3, out_0, out_1, out_2, out_3,
     with ExitStack() as ctx:
         keep = ctx.enter_context(tc.tile_pool(name="keep", bufs=1))
         ring = ctx.enter_context(tc.tile_pool(name="ring", bufs=2))
+        shared = ctx.enter_context(tc.tile_pool(name="shared", bufs=2))
         psum = ctx.enter_context(tc.psum_pool(name="psum", bufs=1))
         ctx.enter_context(tc.manual_schedule())
 
@@ -96,19 +98,19 @@ def tile_evidentialhead_pb_kernel(tc, h_act, W3, b3, out_0, out_1, out_2, out_3,
 
         h_sb, h_t, h_codes, h_scales = {}, {}, {}, {}
         soft, relu, evidence, belief, sort_buf, by_block = {}, {}, {}, {}, {}, {}
-        power, g_bank, m_sq = {}, {}, {}
+        power, g_bank, m_sq, summed, acc = {}, {}, {}, {}, {}
 
         def tiles_of(g):
             return slice(g * GT, (g + 1) * GT)
 
         def load(g, first=0, count=GT):
             if first == 0:
-                h_sb[g] = ring.tile([P, GT, H], BF16, name="h_sb")
+                h_sb[g] = shared.tile([P, GT, H], BF16, name="h_sb", align_bytes=64, offset=0)
             nc.sync.dma_start(out=h_sb[g][:, first : first + count, :], in_=h_rows[:, g * GT + first : g * GT + first + count, :])
 
         def transpose_h(g, which=range(GT), on_vector=()):
             if which[0] == 0:
-                h_t[g] = ring.tile([P, PASSES * GT * P * 4], BF16, name="h_t", align_bytes=64)
+                h_t[g] = shared.tile([P, PASSES * GT * P * 4], BF16, name="h_t", align_bytes=64, offset=2 * GT * H * 2)
             words_out = h_t[g][:].bitcast(F32).rearrange("p (s t r u) -> p s t r u", s=PASSES, t=GT, u=2)
             for t in which:
                 words = h_sb[g][:, t, :].bitcast(F32)
@@ -126,13 +128,21 @@ def tile_evidentialhead_pb_kernel(tc, h_act, W3, b3, out_0, out_1, out_2, out_3,
             h_scales[g] = ring.tile([P, PASSES * GT * P], U8, name="h_scales", align_bytes=64)
             nc.vector.quantize_mx(out=h_codes[g][:].bitcast(E5M2X4), scales=h_scales[g][:], in_=h_t[g][:])
 
+        def quantize_tile(g, t):
+            if t == 0:
+                h_codes[g] = ring.tile([P, PASSES * GT * P], U32, name="h_codes", align_bytes=64)
+                h_scales[g] = ring.tile([P, PASSES * GT * P], U8, name="h_scales", align_bytes=64)
+            for s in range(PASSES):
+                first = (s * GT + t) * P
+                nc.vector.quantize_mx(out=h_codes[g][:, first : first + P].bitcast(E5M2X4), scales=h_scales[g][:, first : first + P], in_=h_t[g][:, 4 * first : 4 * (first + P)])
+
         def logits(g):
-            acc = psum.tile([P, GT * P], F32, name="pair", bufs=2)
+            acc[g] = psum.tile([P, GT * P], F32, name="pair", bufs=2)
             for s in range(PASSES):
                 w_cols = slice(s * K, (s + 1) * K)
                 h_cols = slice(s * GT * P, (s + 1) * GT * P)
                 nc.tensor.matmul_mx(
-                    out=acc[:],
+                    out=acc[g][:],
                     lhsT=w_codes[:, w_cols].bitcast(E4M3X4),
                     lhsT_scale=w_scales[:, w_cols],
                     rhs=h_codes[g][:, h_cols].bitcast(E5M2X4),
@@ -141,9 +151,16 @@ def tile_evidentialhead_pb_kernel(tc, h_act, W3, b3, out_0, out_1, out_2, out_3,
                     stop=(s == PASSES - 1),
                 )
             soft[g] = ring.tile([P, GT * P], F32, name="soft")
+            nc.scalar.activation(out=soft[g][:], in_=acc[g][:], func=ACT.Abs, bias=bias[:])
+
+        def positive_part(g, on_vector=False):
             relu[g] = ring.tile([P, GT * P], F32, name="relu")
-            nc.scalar.activation(out=soft[g][:], in_=acc[:], func=ACT.Abs, bias=bias[:])
-            nc.scalar.activation(out=relu[g][:], in_=acc[:], func=ACT.Relu, bias=bias[:])
+            if on_vector:
+                nc.vector.tensor_scalar(out=relu[g][:], in0=acc[g][:], scalar1=bias[:], scalar2=0.0, op0=ALU.add, op1=ALU.max)
+            else:
+                nc.scalar.activation(out=relu[g][:], in_=acc[g][:], func=ACT.Relu, bias=bias[:])
+
+        def softplus_exp(g):
             nc.scalar.activation(out=soft[g][:], in_=soft[g][:], func=ACT.Exp, scale=-1.0)
 
         def softplus_log(g):
@@ -151,7 +168,7 @@ def tile_evidentialhead_pb_kernel(tc, h_act, W3, b3, out_0, out_1, out_2, out_3,
 
         def evidence_rows_out(g):
             bank = psum.tile([P, GT, K], F32, name="ev_bank")
-            evidence[g] = ring.tile([P, GT, K], F32, name="evidence")
+            evidence[g] = ring.tile([P, GT, K], F32, name="evidence", bufs=4)
             for t in range(GT):
                 cols = slice(t * P, (t + 1) * P)
                 nc.tensor.matmul(bank[:, t, :], lhsT=relu[g][:, cols], rhs=ident[:], is_transpose=True, start=True, stop=False)
@@ -216,11 +233,14 @@ def tile_evidentialhead_pb_kernel(tc, h_act, W3, b3, out_0, out_1, out_2, out_3,
             dst = dst_buf[:].rearrange("p (n w) -> p n w", w=2 * p * GT)[:, :, inner].rearrange("p n (g two q) -> p two n g q", two=2, q=k * GT)
             exchange((dst[:, 0], dst[:, 1]), (src[:, 0], src[:, 1]))
 
-        def copy_ends(g, number, p):
+        def copy_ends(g, number, p, on_vector):
             src_buf, dst_buf = sort_buf[g][number % 2], sort_buf[g][(number + 1) % 2]
             src = src_buf[:].rearrange("p (n f q) -> p n f q", f=4, q=p * GT // 2)[:, :, 0:4:3, :]
             dst = dst_buf[:].rearrange("p (n f q) -> p n f q", f=4, q=p * GT // 2)[:, :, 0:4:3, :]
-            nc.vector.tensor_copy(out=dst, in_=src)
+            if on_vector:
+                nc.vector.tensor_copy(out=dst, in_=src)
+            else:
+                nc.scalar.copy(out=dst, in_=src)
 
         steps = [(1 << a, 1 << b) for a in range(7) for b in range(a, -1, -1)]
 
@@ -258,23 +278,7 @@ def tile_evidentialhead_pb_kernel(tc, h_act, W3, b3, out_0, out_1, out_2, out_3,
         def powers(b, first, last, exponents):
             cols = slice(first * GROUP_COLS, last * GROUP_COLS)
             for n in exponents:
-                if first == 0:
-                    power[b, n] = ring.tile([P, BLOCK_COLS], F32, name="power%d" % n)
-                nc.scalar.activation(out=power[b, n][:, cols], in_=log_step[:, b, first:last, :].rearrange("p g x -> p (g x)"), func=ACT.Exp, scale=float(n))
-
-        def after_logits(j):
-            for g in (2 * j, 2 * j + 1):
-                softplus_log(g)
-            for g in (2 * j, 2 * j + 1):
-                evidence_rows_out(g)
-            for g in (2 * j, 2 * j + 1):
-                alpha_out(g)
-
-        def scaled(j):
-            for g in (2 * j, 2 * j + 1):
-                belief_of(g)
-            for g in (2 * j, 2 * j + 1):
-                prob_out(g)
+                nc.scalar.activation(out=power[b % SLOTS][:, n - 1, cols], in_=log_step[:, b, first:last, :].rearrange("p g x -> p (g x)"), func=ACT.Exp, scale=float(n))
 
         def build_picks():
             place = keep.tile([P, P], F32)
@@ -302,99 +306,135 @@ def tile_evidentialhead_pb_kernel(tc, h_act, W3, b3, out_0, out_1, out_2, out_3,
         nc.vector.tensor_copy(out=w_grouped[:].rearrange("p (s n j) -> p s n j", s=PASSES, j=4), in_=w_raw[:].rearrange("p s j n -> p s n j"))
         transpose_h(0, range(2), on_vector=(1,))
         nc.vector.quantize_mx(out=w_codes[:].bitcast(E4M3X4), scales=w_scales[:], in_=w_grouped[:])
+        quantize_tile(0, 0)
+        quantize_tile(0, 1)
         transpose_h(0, range(2, GT), on_vector=(3,))
         load(2)
-        transpose_h(1, range(1))
-        quantize_h(0)
-        transpose_h(1, range(1, 2), on_vector=(1,))
+        quantize_tile(0, 2)
+        quantize_tile(0, 3)
+        transpose_h(1, range(2), on_vector=(1,))
         logits(0)
+        positive_part(0)
+        softplus_exp(0)
+        quantize_tile(1, 0)
+        quantize_tile(1, 1)
         transpose_h(1, range(2, GT), on_vector=(2, 3))
         load(3)
-        quantize_h(1)
+        quantize_tile(1, 2)
+        quantize_tile(1, 3)
         logits(1)
-        after_logits(0)
+        positive_part(1, on_vector=True)
+        softplus_exp(1)
+        transpose_h(2, on_vector=range(GT))
+        quantize_h(2)
+        softplus_log(0)
+        softplus_log(1)
+        evidence_rows_out(0)
+        evidence_rows_out(1)
         for g in range(2):
             add_classes(tiles_of(g))
             invert(tiles_of(g))
             belief_on_vector(g)
-        for g in range(2):
-            prob_out(g)
-        transpose_h(2)
         transpose_h(3)
 
         all_powers = range(1, DEGREE + 1)
-        halves = (all_powers[: DEGREE // 2], all_powers[DEGREE // 2 :])
+        for slot in range(SLOTS - 1):
+            power[slot] = keep.tile([P, DEGREE, BLOCK_COLS], F32, name="power%d" % slot)
+        last = STAGES - 1
         for j in range(STAGES):
-            if j + 2 < STAGES:
-                load(2 * j + 4)
-                load(2 * j + 5)
-            if j + 1 < STAGES:
-                quantize_h(2 * j + 2)
-                quantize_h(2 * j + 3)
-            if j > 0:
+            behind, ahead, far = j > 0, j < last, j + 1 < last
+            a, b = 2 * j + 2, 2 * j + 3
+            if far:
+                load(a + 2)
+                load(b + 2)
+            if ahead and behind:
+                quantize_h(a)
+                quantize_h(b)
+            if behind:
                 take_logs(j - 1)
-                regroup(j - 1)
-            if j + 1 < STAGES:
-                logits(2 * j + 2)
-                logits(2 * j + 3)
-                after_logits(j + 1)
-            if j > 0:
-                squares(j - 1)
+            if ahead:
+                logits(a)
+                softplus_exp(a)
             for number, (p, k) in enumerate(steps):
                 for g in (2 * j, 2 * j + 1):
                     sort_step(g, number, p, k)
                 if k == p and p > 1:
                     for g in (2 * j, 2 * j + 1):
-                        copy_ends(g, number, p)
-                if number == DL_STEP and j > 0:
+                        copy_ends(g, number, p, not ahead or (not behind and p <= 4))
+                if not behind and (p, k) == (2, 2):
+                    quantize_h(b)
+                if ahead and (p, k) == (2, 2):
+                    positive_part(a)
+                    logits(b)
+                if ahead and (p, k) == (4, 4):
+                    softplus_exp(b)
+                    softplus_log(a)
+                if behind and (p, k) == (4, 2):
                     log_steps(j - 1, 0, BLOCKS)
-                    if j + 1 == STAGES:
-                        for b in range(2):
-                            powers(b, 0, GROUPS - 2, all_powers)
-                if number == RECIP_STEP and j + 1 < STAGES:
+                if ahead and (p, k) == (8, 8):
+                    positive_part(b)
+                    softplus_log(b)
+                    evidence_rows_out(a)
+                if behind and (p, k) == ((8, 8) if ahead else (2, 2)):
+                    regroup(j - 1)
+                if ahead and (p, k) == (16, 16):
+                    evidence_rows_out(b)
+                if behind and (p, k) == ((16, 16) if ahead else (2, 2)):
+                    squares(j - 1)
+                if not behind and (p, k) in ((8, 8), (16, 16)):
+                    alpha_out(p // 16)
+                    prob_out(p // 16)
+                if not ahead and (p, k) == (4, 2):
+                    power[SLOTS - 1] = shared.tile([P, DEGREE, BLOCK_COLS], F32, name="last_slot", bufs=1, align_bytes=64, offset=0)
+                    for slot in range(SLOTS):
+                        powers(slot, 0, GROUPS - 2, all_powers)
+                if ahead and (p, k) == (16, 4):
                     add_classes(stage_cols(j + 1))
-                if number == RECIP_STEP + 1 and j + 1 < STAGES:
+                if ahead and (p, k) == (16, 2):
                     invert(stage_cols(j + 1))
-                    scaled(j + 1)
-                    if j + 2 < STAGES:
-                        transpose_h(2 * j + 4)
-                        transpose_h(2 * j + 5)
-            if j > 0:
+                    belief_of(a)
+                    belief_of(b)
+                if far and (p, k) == (32, 32):
+                    transpose_h(a + 2)
+                    transpose_h(b + 2)
+                if ahead and (p, k) == (64, 64):
+                    for g in (a, b):
+                        alpha_out(g)
+                        prob_out(g)
+            if behind:
                 rank_terms(j - 1)
-        last = STAGES - 1
         take_logs(last)
-        log_steps(last, 0, 2)
-        log_steps(last, 2, BLOCKS)
-        nc.vector.tensor_scalar(out=vacuity[:], in0=inv_s[:], scalar1=float(K), scalar2=None, op0=ALU.mult)
-        nc.sync.dma_start(out=vacuity_rows, in_=vacuity[:])
+        log_steps(last, 0, SLOTS)
         powers(0, GROUPS - 2, GROUPS, all_powers)
         regroup(last)
         powers(1, GROUPS - 2, GROUPS, all_powers)
         squares(last)
         rank_terms(last)
+        powers(2, GROUPS - 2, GROUPS, all_powers)
 
-        def at(b, n, i):
-            return power[b, n][:].rearrange("p (g c t) -> p g c t", c=BLOCK, t=GT)[:, :, i, :]
+        def at(pos, first, count):
+            b, i = divmod(pos, BLOCK)
+            return power[b % SLOTS][:, first - 1 : first - 1 + count, :].rearrange("p n (g c t) -> p (n g) c t", c=BLOCK, t=GT)[:, :, i, :]
 
-        def recur(b, exponents):
-            for i in range(BLOCK):
-                if b == 0 and i == 0:
-                    continue
-                pb, pi = divmod(b * BLOCK + i - 1, BLOCK)
-                for n in exponents:
-                    nc.vector.scalar_tensor_tensor(out=at(b, n, i), in0=at(pb, n, pi), scalar=coef[n], in1=at(b, n, i), op0=ALU.add, op1=ALU.mult)
+        def recur(pos, first, count, seed):
+            nc.vector.scalar_tensor_tensor(out=at(pos, first, count), in0=at(pos - 1, first, count), scalar=seed, in1=at(pos, first, count), op0=ALU.add, op1=ALU.mult)
+
+        def scale(b, n):
+            sums = power[b % SLOTS][:, n - 1, :]
+            nc.scalar.activation(out=sums, in_=sums, func=ACT.Copy, scale=coef[n])
 
         bank_stages = (range(FIRST_BANK), range(FIRST_BANK, STAGES))
 
-        def sum_powers(b, exponents):
-            for n in exponents:
-                for side, members in enumerate(bank_stages):
-                    if n == 1:
-                        g_bank[b, side] = psum.tile([P, len(members), P], F32, name="wide", bufs=4)
-                    for j in members:
-                        nc.tensor.matmul(
-                            g_bank[b, side][:, j - members[0], :], lhsT=power[b, n][:, j * P : (j + 1) * P], rhs=ident[:], is_transpose=True,
-                            start=(n == 1 and j == members[0]), stop=(n == DEGREE and j == members[-1]))
+        def sum_power(b, n):
+            done = summed.get(b, 0)
+            summed[b] = done + 1
+            for side, members in enumerate(bank_stages):
+                if done == 0:
+                    g_bank[b, side] = psum.tile([P, len(members), P], F32, name="wide", bufs=4)
+                for j in members:
+                    nc.tensor.matmul(
+                        g_bank[b, side][:, j - members[0], :], lhsT=power[b % SLOTS][:, n - 1, j * P : (j + 1) * P], rhs=ident[:], is_transpose=True,
+                        start=(done == 0 and j == members[0]), stop=(done == DEGREE - 1 and j == members[-1]))
 
         def weigh(b):
             for side, members in enumerate(bank_stages):
@@ -405,14 +445,35 @@ def tile_evidentialhead_pb_kernel(tc, h_act, W3, b3, out_0, out_1, out_2, out_3,
                 for j in members:
                     nc.tensor.matmul(total[:, stage_cols(j)], lhsT=prod[:, j - members[0], :], rhs=pick[:], start=False, stop=(b == BLOCKS - 1 and j == last))
 
-        for b in range(BLOCKS):
-            for side, exponents in enumerate(halves):
-                recur(b, exponents)
-                if side == 0 and b > 0:
-                    weigh(b - 1)
-                sum_powers(b, exponents)
-                if 1 <= b < BLOCKS - 1:
-                    powers(b + 1, 0, GROUPS, exponents)
+        delay = [lane * BLOCK // LANES for lane in range(LANES)]
+        joint_end = K - BLOCK
+        for step in range(1, K + BLOCK + delay[-1]):
+            b, i = divmod(step, BLOCK)
+            if step < joint_end:
+                recur(step, 1, JOINT, 1.0)
+            for lane in range(LANES):
+                pos = step - delay[lane]
+                n = JOINT + 1 + lane
+                if pos >= K:
+                    pos, n = pos - BLOCK, lane + 1
+                if 1 <= pos < K:
+                    recur(pos, n, 1, coef[n])
+                    if pos % BLOCK == BLOCK - 1:
+                        sum_power(pos // BLOCK, n)
+                    if pos % BLOCK == 1 and n > JOINT and 1 <= pos // BLOCK <= BLOCKS - SLOTS:
+                        powers(pos // BLOCK + SLOTS - 1, 0, GROUPS, (n,))
+            if step == 1:
+                log_steps(last, SLOTS, BLOCKS)
+            if step == 2:
+                nc.vector.tensor_scalar(out=vacuity[:], in0=inv_s[:], scalar1=float(K), scalar2=None, op0=ALU.mult)
+                nc.sync.dma_start(out=vacuity_rows, in_=vacuity[:])
+            if 1 <= b < BLOCKS and i < JOINT:
+                scale(b - 1, i + 1)
+                sum_power(b - 1, i + 1)
+            if 1 <= b <= BLOCKS - SLOTS and BLOCK // 2 <= i < BLOCK // 2 + JOINT:
+                powers(b + SLOTS - 1, 0, GROUPS, (i - BLOCK // 2 + 1,))
+            if 1 <= b < BLOCKS and i == BLOCK - 1:
+                weigh(b - 1)
         weigh(BLOCKS - 1)
         nc.vector.tensor_scalar(out=dissonance[:], in0=total[:], scalar1=-m_bias * m_bias * pairs, scalar2=None, op0=ALU.add)
         nc.sync.dma_start(out=dissonance_rows, in_=dissonance[:])

@@ -33,6 +33,8 @@ FIRST_BANK = 3
 JOINT = 6
 LANES = DEGREE - JOINT
 SLOTS = 3
+SUM_LAG = 3
+WEIGH_AT = 4
 ABOVE_ALL = 128.0
 
 
@@ -88,6 +90,8 @@ def tile_evidentialhead_pb_kernel(tc, h_act, W3, b3, out_0, out_1, out_2, out_3,
         strength = keep.tile([P, TILES], F32)
         inv_s = keep.tile([P, TILES], F32)
         vacuity = keep.tile([P, TILES], F32)
+        rank_sum = keep.tile([P, TILES], F32)
+        ratio_sum = keep.tile([P, TILES], F32)
         dissonance = keep.tile([P, TILES], F32)
         u_sq = keep.tile([P, BLOCKS, STAGES, P], F32)
         log_step = keep.tile([P, BLOCKS, GROUPS, GROUP_COLS], F32)
@@ -98,7 +102,7 @@ def tile_evidentialhead_pb_kernel(tc, h_act, W3, b3, out_0, out_1, out_2, out_3,
 
         h_sb, h_t, h_codes, h_scales = {}, {}, {}, {}
         soft, relu, evidence, belief, sort_buf, by_block = {}, {}, {}, {}, {}, {}
-        power, g_bank, m_sq, summed, acc = {}, {}, {}, {}, {}
+        power, g_bank, m_sq, summed, acc, back = {}, {}, {}, {}, {}, {}
 
         def tiles_of(g):
             return slice(g * GT, (g + 1) * GT)
@@ -233,14 +237,11 @@ def tile_evidentialhead_pb_kernel(tc, h_act, W3, b3, out_0, out_1, out_2, out_3,
             dst = dst_buf[:].rearrange("p (n w) -> p n w", w=2 * p * GT)[:, :, inner].rearrange("p n (g two q) -> p two n g q", two=2, q=k * GT)
             exchange((dst[:, 0], dst[:, 1]), (src[:, 0], src[:, 1]))
 
-        def copy_ends(g, number, p, on_vector):
+        def copy_ends(g, number, p):
             src_buf, dst_buf = sort_buf[g][number % 2], sort_buf[g][(number + 1) % 2]
             src = src_buf[:].rearrange("p (n f q) -> p n f q", f=4, q=p * GT // 2)[:, :, 0:4:3, :]
             dst = dst_buf[:].rearrange("p (n f q) -> p n f q", f=4, q=p * GT // 2)[:, :, 0:4:3, :]
-            if on_vector:
-                nc.vector.tensor_copy(out=dst, in_=src)
-            else:
-                nc.scalar.copy(out=dst, in_=src)
+            nc.vector.tensor_copy(out=dst, in_=src)
 
         steps = [(1 << a, 1 << b) for a in range(7) for b in range(a, -1, -1)]
 
@@ -273,7 +274,7 @@ def tile_evidentialhead_pb_kernel(tc, h_act, W3, b3, out_0, out_1, out_2, out_3,
 
         def rank_terms(j):
             for b in range(BLOCKS):
-                nc.tensor.matmul(total[:, stage_cols(j)], lhsT=m_sq[j][:, b, :], rhs=pick_rank[:, b, :], start=(j == 0 and b == 0), stop=False)
+                nc.tensor.matmul(total[:, stage_cols(j)], lhsT=m_sq[j][:, b, :], rhs=pick_rank[:, b, :], start=(j == 0 and b == 0), stop=(j == STAGES - 1 and b == BLOCKS - 1))
 
         def powers(b, first, last, exponents):
             cols = slice(first * GROUP_COLS, last * GROUP_COLS)
@@ -360,7 +361,7 @@ def tile_evidentialhead_pb_kernel(tc, h_act, W3, b3, out_0, out_1, out_2, out_3,
                     sort_step(g, number, p, k)
                 if k == p and p > 1:
                     for g in (2 * j, 2 * j + 1):
-                        copy_ends(g, number, p, not ahead or (not behind and p <= 4))
+                        copy_ends(g, number, p)
                 if not behind and (p, k) == (2, 2):
                     quantize_h(b)
                 if ahead and (p, k) == (2, 2):
@@ -442,8 +443,12 @@ def tile_evidentialhead_pb_kernel(tc, h_act, W3, b3, out_0, out_1, out_2, out_3,
                 nc.vector.scalar_tensor_tensor(
                     out=prod[:].rearrange("p i r -> p (i r)"), in0=u_sq[:, b, members[0] : members[-1] + 1, :].rearrange("p i r -> p (i r)"), scalar=-half_eps * half_eps,
                     in1=g_bank[b, side][:].rearrange("p i r -> p (i r)"), op0=ALU.add, op1=ALU.mult)
+                if b == 0:
+                    back[side] = psum.tile([P, len(members), P], F32, name="pair", bufs=2)
                 for j in members:
-                    nc.tensor.matmul(total[:, stage_cols(j)], lhsT=prod[:, j - members[0], :], rhs=pick[:], start=False, stop=(b == BLOCKS - 1 and j == last))
+                    nc.tensor.matmul(
+                        back[side][:, j - members[0], :], lhsT=prod[:, j - members[0], :], rhs=ident[:], is_transpose=True,
+                        start=(b == 0 and j == members[0]), stop=(b == BLOCKS - 1 and j == members[-1]))
 
         delay = [lane * BLOCK // LANES for lane in range(LANES)]
         joint_end = K - BLOCK
@@ -460,7 +465,7 @@ def tile_evidentialhead_pb_kernel(tc, h_act, W3, b3, out_0, out_1, out_2, out_3,
                     recur(pos, n, 1, coef[n])
                     if pos % BLOCK == BLOCK - 1:
                         sum_power(pos // BLOCK, n)
-                    if pos % BLOCK == 1 and n > JOINT and 1 <= pos // BLOCK <= BLOCKS - SLOTS:
+                    if pos % BLOCK == JOINT and n > JOINT and 1 <= pos // BLOCK <= BLOCKS - SLOTS:
                         powers(pos // BLOCK + SLOTS - 1, 0, GROUPS, (n,))
             if step == 1:
                 log_steps(last, SLOTS, BLOCKS)
@@ -469,11 +474,19 @@ def tile_evidentialhead_pb_kernel(tc, h_act, W3, b3, out_0, out_1, out_2, out_3,
                 nc.sync.dma_start(out=vacuity_rows, in_=vacuity[:])
             if 1 <= b < BLOCKS and i < JOINT:
                 scale(b - 1, i + 1)
-                sum_power(b - 1, i + 1)
-            if 1 <= b <= BLOCKS - SLOTS and BLOCK // 2 <= i < BLOCK // 2 + JOINT:
-                powers(b + SLOTS - 1, 0, GROUPS, (i - BLOCK // 2 + 1,))
-            if 1 <= b < BLOCKS and i == BLOCK - 1:
-                weigh(b - 1)
+            if 1 <= b < BLOCKS and SUM_LAG <= i < SUM_LAG + JOINT:
+                sum_power(b - 1, i - SUM_LAG + 1)
+            if 1 <= b <= BLOCKS - SLOTS and BLOCK - JOINT <= i:
+                powers(b + SLOTS - 1, 0, GROUPS, (i - (BLOCK - JOINT) + 1,))
+            if 2 <= b <= BLOCKS and i == WEIGH_AT:
+                weigh(b - 2)
+            if step == BLOCK:
+                nc.vector.tensor_scalar(out=rank_sum[:], in0=total[:], scalar1=-m_bias * m_bias * pairs, scalar2=None, op0=ALU.add)
         weigh(BLOCKS - 1)
-        nc.vector.tensor_scalar(out=dissonance[:], in0=total[:], scalar1=-m_bias * m_bias * pairs, scalar2=None, op0=ALU.add)
+        for side, members in enumerate(bank_stages):
+            cols = slice(members[0] * 2 * GT, (members[-1] + 1) * 2 * GT)
+            nc.vector.tensor_reduce(
+                out=ratio_sum[:, cols].rearrange("p (g t) -> p g t", t=GT), in_=back[side][:].rearrange("p j (i c t) -> p (j i) t c", i=2, t=GT),
+                axis=mybir.AxisListType.X, op=ALU.add)
+        nc.vector.tensor_tensor(out=dissonance[:], in0=ratio_sum[:], in1=rank_sum[:], op=ALU.add)
         nc.sync.dma_start(out=dissonance_rows, in_=dissonance[:])

import math
from contextlib import ExitStack

import concourse.mybir as mybir
from concourse.masks import make_identity

ROWS, H, K = 5120, 1024, 128
EPS = 1e-8
FLOPS = 2 * ROWS * H * K

F32 = mybir.dt.float32
BF16 = mybir.dt.bfloat16
U32 = mybir.dt.uint32
U8 = mybir.dt.uint8
E5M2X4 = mybir.dt.float8_e5m2_x4
E4M3X4 = mybir.dt.float8_e4m3fn_x4
ACT = mybir.ActivationFunctionType
ALU = mybir.AluOpType

P = 128
TILES = ROWS // P
GT = 4
GROUPS = TILES // GT
STAGES = GROUPS // 2
PASSES = H // 512
DEGREE = 12
BLOCK = 16
BLOCKS = K // BLOCK
GROUP_COLS = BLOCK * GT
BLOCK_COLS = GROUPS * GROUP_COLS
BANK_CHUNKS = 4
FIRST_BANK = 3
JOINT = 6
LANES = DEGREE - JOINT
SLOTS = 3
SUM_LAG = 3
WEIGH_AT = 4
ABOVE_ALL = 128.0


def ratio_polynomial(degree):
    rho = 3.0 - math.sqrt(8.0)
    cheb = [[1.0], [-1.0, 2.0]]
    for n in range(2, degree + 1):
        nxt = [0.0] * (n + 1)
        for i, v in enumerate(cheb[n - 1]):
            nxt[i] -= 2.0 * v
            nxt[i + 1] += 4.0 * v
        for i, v in enumerate(cheb[n - 2]):
            nxt[i] -= v
        cheb.append(nxt)
    coef = [0.0] * (degree + 1)
    for n in range(degree + 1):
        weight = 4.0 / math.sqrt(8.0) * (1.0 if n == 0 else 2.0) * (-rho) ** n
        for i, v in enumerate(cheb[n]):
            coef[i] += weight * v
    coef[0] -= 1.0
    return coef


def tile_evidentialhead_pb_kernel(tc, h_act, W3, b3, out_0, out_1, out_2, out_3, out_4):
    nc = tc.nc
    coef = ratio_polynomial(DEGREE)
    half_eps = EPS / 2
    m_scale = math.sqrt(1.0 + coef[0])
    m_bias = m_scale * EPS * coef[0] / (1.0 + coef[0]) / 2
    pairs = K * (K - 1) // 2

    h_rows = h_act.rearrange("(p t) k -> p t k", t=TILES)
    alpha_rows = out_0.rearrange("(p t) c -> p t c", t=TILES)
    evidence_rows = out_1.rearrange("(p t) c -> p t c", t=TILES)
    prob_rows = out_2.rearrange("(p t) c -> p t c", t=TILES)
    vacuity_rows = out_3.rearrange("(p t) -> p t", t=TILES)
    dissonance_rows = out_4.rearrange("(p t) -> p t", t=TILES)

    with ExitStack() as ctx:
        keep = ctx.enter_context(tc.tile_pool(name="keep", bufs=1))
        ring = ctx.enter_context(tc.tile_pool(name="ring", bufs=2))
        shared = ctx.enter_context(tc.tile_pool(name="shared", bufs=2))
        psum = ctx.enter_context(tc.psum_pool(name="psum", bufs=1))
        ctx.enter_context(tc.manual_schedule())

        ident = keep.tile([P, P], F32)
        w_raw = keep.tile([P, PASSES, 4, K], BF16)
        w_grouped = keep.tile([P, PASSES * K * 4], BF16, align_bytes=64)
        w_codes = keep.tile([P, PASSES * K], U32, align_bytes=64)
        w_scales = keep.tile([P, PASSES * K], U8, align_bytes=64)
        bias = keep.tile([P, 1], BF16)
        ev_sum = keep.tile([P, TILES], F32)
        strength = keep.tile([P, TILES], F32)
        inv_s = keep.tile([P, TILES], F32)
        vacuity = keep.tile([P, TILES], F32)
        rank_sum = keep.tile([P, TILES], F32)
        ratio_sum = keep.tile([P, TILES], F32)
        dissonance = keep.tile([P, TILES], F32)
        u_sq = keep.tile([P, BLOCKS, STAGES, P], F32)
        log_step = keep.tile([P, BLOCKS, GROUPS, GROUP_COLS], F32)
        log_u = keep.tile([P, 2, GT + K * GT], F32)
        pick = keep.tile([P, 2 * GT], F32)
        pick_rank = keep.tile([P, BLOCKS, 2 * GT], F32)
        total = psum.tile([P, TILES], F32, name="total")

        h_sb, h_t, h_codes, h_scales = {}, {}, {}, {}
        soft, relu, evidence, belief, sort_buf, by_block = {}, {}, {}, {}, {}, {}
        power, g_bank, m_sq, summed, acc, back = {}, {}, {}, {}, {}, {}

        def tiles_of(g):
            return slice(g * GT, (g + 1) * GT)

        def load(g, first=0, count=GT):
            if first == 0:
                h_sb[g] = shared.tile([P, GT, H], BF16, name="h_sb", align_bytes=64, offset=0)
            nc.sync.dma_start(out=h_sb[g][:, first : first + count, :], in_=h_rows[:, g * GT + first : g * GT + first + count, :])

        def transpose_h(g, which=range(GT), on_vector=()):
            if which[0] == 0:
                h_t[g] = shared.tile([P, PASSES * GT * P * 4], BF16, name="h_t", align_bytes=64, offset=2 * GT * H * 2)
            words_out = h_t[g][:].bitcast(F32).rearrange("p (s t r u) -> p s t r u", s=PASSES, t=GT, u=2)
            for t in which:
                words = h_sb[g][:, t, :].bitcast(F32)
                bank = psum.tile([P, PASSES, 2, P], F32, name="wide", bufs=4)
                for s in range(PASSES):
                    for u in range(2):
                        nc.tensor.transpose(bank[:, s, u, :], words[:, 256 * s + u : 256 * (s + 1) : 2], ident[:])
                if t in on_vector:
                    nc.vector.tensor_copy(out=words_out[:, :, t, :, :], in_=bank[:].rearrange("p s u r -> p s r u"))
                else:
                    nc.scalar.copy(out=words_out[:, :, t, :, :], in_=bank[:].rearrange("p s u r -> p s r u"))

        def quantize_h(g):
            h_codes[g] = ring.tile([P, PASSES * GT * P], U32, name="h_codes", align_bytes=64)
            h_scales[g] = ring.tile([P, PASSES * GT * P], U8, name="h_scales", align_bytes=64)
            nc.vector.quantize_mx(out=h_codes[g][:].bitcast(E5M2X4), scales=h_scales[g][:], in_=h_t[g][:])

        def quantize_tile(g, t):
            if t == 0:
                h_codes[g] = ring.tile([P, PASSES * GT * P], U32, name="h_codes", align_bytes=64)
                h_scales[g] = ring.tile([P, PASSES * GT * P], U8, name="h_scales", align_bytes=64)
            for s in range(PASSES):
                first = (s * GT + t) * P
                nc.vector.quantize_mx(out=h_codes[g][:, first : first + P].bitcast(E5M2X4), scales=h_scales[g][:, first : first + P], in_=h_t[g][:, 4 * first : 4 * (first + P)])

        def logits(g):
            acc[g] = psum.tile([P, GT * P], F32, name="pair", bufs=2)
            for s in range(PASSES):
                w_cols = slice(s * K, (s + 1) * K)
                h_cols = slice(s * GT * P, (s + 1) * GT * P)
                nc.tensor.matmul_mx(
                    out=acc[g][:],
                    lhsT=w_codes[:, w_cols].bitcast(E4M3X4),
                    lhsT_scale=w_scales[:, w_cols],
                    rhs=h_codes[g][:, h_cols].bitcast(E5M2X4),
                    rhs_scale=h_scales[g][:, h_cols],
                    start=(s == 0),
                    stop=(s == PASSES - 1),
                )
            soft[g] = ring.tile([P, GT * P], F32, name="soft")
            nc.scalar.activation(out=soft[g][:], in_=acc[g][:], func=ACT.Abs, bias=bias[:])

        def positive_part(g, on_vector=False):
            relu[g] = ring.tile([P, GT * P], F32, name="relu")
            if on_vector:
                nc.vector.tensor_scalar(out=relu[g][:], in0=acc[g][:], scalar1=bias[:], scalar2=0.0, op0=ALU.add, op1=ALU.max)
            else:
                nc.scalar.activation(out=relu[g][:], in_=acc[g][:], func=ACT.Relu, bias=bias[:])

        def softplus_exp(g):
            nc.scalar.activation(out=soft[g][:], in_=soft[g][:], func=ACT.Exp, scale=-1.0)

        def softplus_log(g):
            nc.scalar.activation(out=soft[g][:], in_=soft[g][:], func=ACT.Ln, bias=1.0)

        def evidence_rows_out(g):
            bank = psum.tile([P, GT, K], F32, name="ev_bank")
            evidence[g] = ring.tile([P, GT, K], F32, name="evidence", bufs=4)
            for t in range(GT):
                cols = slice(t * P, (t + 1) * P)
                nc.tensor.matmul(bank[:, t, :], lhsT=relu[g][:, cols], rhs=ident[:], is_transpose=True, start=True, stop=False)
                nc.tensor.matmul(bank[:, t, :], lhsT=soft[g][:, cols], rhs=ident[:], is_transpose=True, start=False, stop=True)
            for t in range(GT):
                col = g * GT + t
                nc.scalar.activation(out=evidence[g][:, t, :], in_=bank[:, t, :], func=ACT.Identity, accum_out=ev_sum[:, col : col + 1])
            nc.sync.dma_start(out=evidence_rows[:, tiles_of(g), :], in_=evidence[g][:])

        def alpha_out(g):
            alpha = ring.tile([P, GT, K], F32, name="alpha")
            nc.scalar.activation(out=alpha[:], in_=evidence[g][:], func=ACT.Identity, bias=1.0)
            nc.sync.dma_start(out=alpha_rows[:, tiles_of(g), :], in_=alpha[:])

        def stage_cols(j):
            return slice(2 * j * GT, 2 * (j + 1) * GT)

        def add_classes(cols):
            nc.vector.tensor_scalar(out=strength[:, cols], in0=ev_sum[:, cols], scalar1=float(K), scalar2=None, op0=ALU.add)

        def invert(cols):
            nc.vector.reciprocal(out=inv_s[:, cols], in_=strength[:, cols])

        def belief_on_vector(g):
            belief[g] = ring.tile([P, GT, K], F32, name="belief", bufs=4)
            nc.vector.tensor_tensor(out=belief[g][:], in0=evidence[g][:], in1=inv_s[:, tiles_of(g)].unsqueeze(2).to_broadcast([P, GT, K]), op=ALU.mult)

        def belief_of(g):
            belief[g] = ring.tile([P, GT, K], F32, name="belief", bufs=4)
            for t in range(GT):
                col = g * GT + t
                nc.scalar.activation(out=belief[g][:, t, :], in_=evidence[g][:, t, :], func=ACT.Copy, scale=inv_s[:, col : col + 1])

        def prob_out(g):
            prob = ring.tile([P, GT, K], F32, name="prob")
            for t in range(GT):
                col = g * GT + t
                nc.scalar.activation(out=prob[:, t, :], in_=evidence[g][:, t, :], func=ACT.Identity, scale=inv_s[:, col : col + 1], bias=inv_s[:, col : col + 1])
            nc.sync.dma_start(out=prob_rows[:, tiles_of(g), :], in_=prob[:])

        def exchange(dst, src):
            nc.vector.tensor_tensor(out=dst[0], in0=src[0], in1=src[1], op=ALU.max)
            nc.vector.tensor_tensor(out=dst[1], in0=src[0], in1=src[1], op=ALU.min)

        def sort_step(g, number, p, k):
            if number == 0:
                first = ring.tile([P, K * GT], F32, name="sort_a", bufs=4)
                second = ring.tile([P, K * GT], F32, name="sort_b", bufs=2)
                sort_buf[g] = (second, first)
                src = belief[g][:].rearrange("p t (two c) -> p two c t", two=2)
                dst = second[:].rearrange("p (c two t) -> p two c t", two=2, t=GT)
                exchange((dst[:, 0], dst[:, 1]), (src[:, 0], src[:, 1]))
                return
            src_buf, dst_buf = sort_buf[g][(number - 1) % 2], sort_buf[g][number % 2]
            if k == p:
                src = src_buf[:].rearrange("p (n two q) -> p two n q", two=2, q=p * GT)
                dst = dst_buf[:].rearrange("p (n two q) -> p two n q", two=2, q=p * GT)
                exchange((dst[:, 0], dst[:, 1]), (src[:, 0], src[:, 1]))
                return
            inner = slice(k * GT, (2 * p - k) * GT)
            src = src_buf[:].rearrange("p (n w) -> p n w", w=2 * p * GT)[:, :, inner].rearrange("p n (g two q) -> p two n g q", two=2, q=k * GT)
            dst = dst_buf[:].rearrange("p (n w) -> p n w", w=2 * p * GT)[:, :, inner].rearrange("p n (g two q) -> p two n g q", two=2, q=k * GT)
            exchange((dst[:, 0], dst[:, 1]), (src[:, 0], src[:, 1]))

        def copy_ends(g, number, p):
            src_buf, dst_buf = sort_buf[g][number % 2], sort_buf[g][(number + 1) % 2]
            src = src_buf[:].rearrange("p (n f q) -> p n f q", f=4, q=p * GT // 2)[:, :, 0:4:3, :]
            dst = dst_buf[:].rearrange("p (n f q) -> p n f q", f=4, q=p * GT // 2)[:, :, 0:4:3, :]
            nc.vector.tensor_copy(out=dst, in_=src)

        steps = [(1 << a, 1 << b) for a in range(7) for b in range(a, -1, -1)]

        def sorted_of(g):
            return sort_buf[g][(len(steps) - 1) % 2]

        def take_logs(j):
            for i in range(2):
                nc.scalar.activation(out=log_u[:, i, GT:], in_=sorted_of(2 * j + i)[:], func=ACT.Ln, bias=half_eps)

        def regroup(j):
            by_block[j] = ring.tile([P, BLOCKS, 2, GROUP_COLS], F32, name="by_block", bufs=1)
            for i in range(2):
                nc.scalar.copy(out=by_block[j][:, :, i, :], in_=sorted_of(2 * j + i)[:].rearrange("p (b x) -> p b x", x=GROUP_COLS))

        def log_steps(j, first, last):
            cols = slice(first * GROUP_COLS, last * GROUP_COLS)
            below = log_u[:, :, GT:][:, :, cols].rearrange("p i (b x) -> p b i x", x=GROUP_COLS)
            above = log_u[:, :, : K * GT][:, :, cols].rearrange("p i (b x) -> p b i x", x=GROUP_COLS)
            nc.vector.tensor_tensor(out=log_step[:, first:last, 2 * j : 2 * j + 2, :], in0=below, in1=above, op=ALU.subtract)

        def squares(j):
            m_sq[j] = ring.tile([P, BLOCKS, P], F32, name="m_sq", bufs=1)
            for first in range(0, BLOCKS, BANK_CHUNKS):
                bank = psum.tile([P, BANK_CHUNKS, P], F32, name="pair", bufs=2)
                for i in range(BANK_CHUNKS):
                    nc.tensor.transpose(bank[:, i, :], by_block[j][:, first + i, :, :].rearrange("p i x -> p (i x)"), ident[:])
                nc.scalar.activation(out=u_sq[:, first : first + BANK_CHUNKS, j, :], in_=bank[:], func=ACT.Square, bias=half_eps)
                nc.scalar.activation(out=m_sq[j][:, first : first + BANK_CHUNKS, :], in_=bank[:], func=ACT.Square, scale=m_scale, bias=m_bias)

        def rank_terms(j):
            for b in range(BLOCKS):
                nc.tensor.matmul(total[:, stage_cols(j)], lhsT=m_sq[j][:, b, :], rhs=pick_rank[:, b, :], start=(j == 0 and b == 0), stop=(j == STAGES - 1 and b == BLOCKS - 1))

        def powers(b, first, last, exponents):
            cols = slice(first * GROUP_COLS, last * GROUP_COLS)
            for n in exponents:
                nc.scalar.activation(out=power[b % SLOTS][:, n - 1, cols], in_=log_step[:, b, first:last, :].rearrange("p g x -> p (g x)"), func=ACT.Exp, scale=float(n))

        def build_picks():
            place = keep.tile([P, P], F32)
            local = keep.tile([P, 1], F32)
            rank = keep.tile([P, BLOCKS], F32)
            nc.gpsimd.iota(place[:], [[0, 2], [1, BLOCK], [0, GT]], base=0, channel_multiplier=0, allow_small_or_imprecise_dtypes=True)
            nc.gpsimd.iota(rank[:], [[BLOCK, BLOCKS]], base=0, channel_multiplier=0, allow_small_or_imprecise_dtypes=True)
            nc.vector.tensor_tensor(out=place[:], in0=place[:], in1=ident[:], op=ALU.mult)
            nc.vector.tensor_reduce(out=pick[:].rearrange("p (i t) -> p i t", t=GT), in_=ident[:].rearrange("p (i c t) -> p i t c", i=2, t=GT), axis=mybir.AxisListType.X, op=ALU.add)
            nc.vector.tensor_reduce(out=local[:], in_=place[:], axis=mybir.AxisListType.X, op=ALU.add)
            nc.vector.tensor_scalar(out=rank[:], in0=rank[:], scalar1=local[:], scalar2=None, op0=ALU.add)
            shape = [P, BLOCKS, 2 * GT]
            nc.vector.tensor_tensor(out=pick_rank[:], in0=pick[:].unsqueeze(1).to_broadcast(shape), in1=rank[:].unsqueeze(2).to_broadcast(shape), op=ALU.mult)

        make_identity(nc, ident[:])
        nc.gpsimd.memset(log_u[:, :, :GT], ABOVE_ALL)
        load(0, 0, 1)
        nc.sync.dma_start(out=w_raw[:], in_=W3.rearrange("(s p j) n -> p s j n", s=PASSES, j=4))
        nc.sync.dma_start(out=bias[:], in_=b3.rearrange("(p o) -> p o", o=1))
        for t in range(1, GT):
            load(0, t, 1)
        load(1, 0, 2)
        load(1, 2, 2)
        build_picks()
        nc.vector.tensor_copy(out=w_grouped[:].rearrange("p (s n j) -> p s n j", s=PASSES, j=4), in_=w_raw[:].rearrange("p s j n -> p s n j"))
        transpose_h(0, range(2), on_vector=(1,))
        nc.vector.quantize_mx(out=w_codes[:].bitcast(E4M3X4), scales=w_scales[:], in_=w_grouped[:])
        quantize_tile(0, 0)
        quantize_tile(0, 1)
        transpose_h(0, range(2, GT), on_vector=(3,))
        load(2)
        quantize_tile(0, 2)
        quantize_tile(0, 3)
        transpose_h(1, range(2), on_vector=(1,))
        logits(0)
        positive_part(0)
        softplus_exp(0)
        quantize_tile(1, 0)
        quantize_tile(1, 1)
        transpose_h(1, range(2, GT), on_vector=(2, 3))
        load(3)
        quantize_tile(1, 2)
        quantize_tile(1, 3)
        logits(1)
        positive_part(1, on_vector=True)
        softplus_exp(1)
        transpose_h(2, on_vector=range(GT))
        quantize_h(2)
        softplus_log(0)
        softplus_log(1)
        evidence_rows_out(0)
        evidence_rows_out(1)
        for g in range(2):
            add_classes(tiles_of(g))
            invert(tiles_of(g))
            belief_on_vector(g)
        transpose_h(3)

        all_powers = range(1, DEGREE + 1)
        for slot in range(SLOTS - 1):
            power[slot] = keep.tile([P, DEGREE, BLOCK_COLS], F32, name="power%d" % slot)
        last = STAGES - 1
        for j in range(STAGES):
            behind, ahead, far = j > 0, j < last, j + 1 < last
            a, b = 2 * j + 2, 2 * j + 3
            if far:
                load(a + 2)
                load(b + 2)
            if ahead and behind:
                quantize_h(a)
                quantize_h(b)
            if behind:
                take_logs(j - 1)
            if ahead:
                logits(a)
                softplus_exp(a)
            for number, (p, k) in enumerate(steps):
                for g in (2 * j, 2 * j + 1):
                    sort_step(g, number, p, k)
                if k == p and p > 1:
                    for g in (2 * j, 2 * j + 1):
                        copy_ends(g, number, p)
                if not behind and (p, k) == (2, 2):
                    quantize_h(b)
                if ahead and (p, k) == (2, 2):
                    positive_part(a)
                    logits(b)
                if ahead and (p, k) == (4, 4):
                    softplus_exp(b)
                    softplus_log(a)
                if behind and (p, k) == (4, 2):
                    log_steps(j - 1, 0, BLOCKS)
                if ahead and (p, k) == (8, 8):
                    positive_part(b)
                    softplus_log(b)
                    evidence_rows_out(a)
                if behind and (p, k) == ((8, 8) if ahead else (2, 2)):
                    regroup(j - 1)
                if ahead and (p, k) == (16, 16):
                    evidence_rows_out(b)
                if behind and (p, k) == ((16, 16) if ahead else (2, 2)):
                    squares(j - 1)
                if not behind and (p, k) in ((8, 8), (16, 16)):
                    alpha_out(p // 16)
                    prob_out(p // 16)
                if not ahead and (p, k) == (4, 2):
                    power[SLOTS - 1] = shared.tile([P, DEGREE, BLOCK_COLS], F32, name="last_slot", bufs=1, align_bytes=64, offset=0)
                    for slot in range(SLOTS):
                        powers(slot, 0, GROUPS - 2, all_powers)
                if ahead and (p, k) == (16, 4):
                    add_classes(stage_cols(j + 1))
                if ahead and (p, k) == (16, 2):
                    invert(stage_cols(j + 1))
                    belief_of(a)
                    belief_of(b)
                if far and (p, k) == (32, 32):
                    transpose_h(a + 2)
                    transpose_h(b + 2)
                if ahead and (p, k) == (64, 64):
                    for g in (a, b):
                        alpha_out(g)
                        prob_out(g)
            if behind:
                rank_terms(j - 1)
        take_logs(last)
        log_steps(last, 0, SLOTS)
        powers(0, GROUPS - 2, GROUPS, all_powers)
        regroup(last)
        powers(1, GROUPS - 2, GROUPS, all_powers)
        squares(last)
        rank_terms(last)
        powers(2, GROUPS - 2, GROUPS, all_powers)

        def at(pos, first, count):
            b, i = divmod(pos, BLOCK)
            return power[b % SLOTS][:, first - 1 : first - 1 + count, :].rearrange("p n (g c t) -> p (n g) c t", c=BLOCK, t=GT)[:, :, i, :]

        def recur(pos, first, count, seed):
            nc.vector.scalar_tensor_tensor(out=at(pos, first, count), in0=at(pos - 1, first, count), scalar=seed, in1=at(pos, first, count), op0=ALU.add, op1=ALU.mult)

        def scale(b, n):
            sums = power[b % SLOTS][:, n - 1, :]
            nc.scalar.activation(out=sums, in_=sums, func=ACT.Copy, scale=coef[n])

        bank_stages = (range(FIRST_BANK), range(FIRST_BANK, STAGES))

        def sum_power(b, n):
            done = summed.get(b, 0)
            summed[b] = done + 1
            for side, members in enumerate(bank_stages):
                if done == 0:
                    g_bank[b, side] = psum.tile([P, len(members), P], F32, name="wide", bufs=4)
                for j in members:
                    nc.tensor.matmul(
                        g_bank[b, side][:, j - members[0], :], lhsT=power[b % SLOTS][:, n - 1, j * P : (j + 1) * P], rhs=ident[:], is_transpose=True,
                        start=(done == 0 and j == members[0]), stop=(done == DEGREE - 1 and j == members[-1]))

        def weigh(b):
            for side, members in enumerate(bank_stages):
                prod = ring.tile([P, len(members), P], F32, name="prod")
                nc.vector.scalar_tensor_tensor(
                    out=prod[:].rearrange("p i r -> p (i r)"), in0=u_sq[:, b, members[0] : members[-1] + 1, :].rearrange("p i r -> p (i r)"), scalar=-half_eps * half_eps,
                    in1=g_bank[b, side][:].rearrange("p i r -> p (i r)"), op0=ALU.add, op1=ALU.mult)
                if b == 0:
                    back[side] = psum.tile([P, len(members), P], F32, name="pair", bufs=2)
                for j in members:
                    nc.tensor.matmul(
                        back[side][:, j - members[0], :], lhsT=prod[:, j - members[0], :], rhs=ident[:], is_transpose=True,
                        start=(b == 0 and j == members[0]), stop=(b == BLOCKS - 1 and j == members[-1]))

        delay = [lane * BLOCK // LANES for lane in range(LANES)]
        joint_end = K - BLOCK
        for step in range(1, K + BLOCK + delay[-1]):
            b, i = divmod(step, BLOCK)
            if step < joint_end:
                recur(step, 1, JOINT, 1.0)
            for lane in range(LANES):
                pos = step - delay[lane]
                n = JOINT + 1 + lane
                if pos >= K:
                    pos, n = pos - BLOCK, lane + 1
                if 1 <= pos < K:
                    recur(pos, n, 1, coef[n])
                    if pos % BLOCK == BLOCK - 1:
                        sum_power(pos // BLOCK, n)
                    if pos % BLOCK == JOINT and n > JOINT and 1 <= pos // BLOCK <= BLOCKS - SLOTS:
                        powers(pos // BLOCK + SLOTS - 1, 0, GROUPS, (n,))
            if step == 1:
                log_steps(last, SLOTS, BLOCKS)
            if step == 2:
                nc.vector.tensor_scalar(out=vacuity[:], in0=inv_s[:], scalar1=float(K), scalar2=None, op0=ALU.mult)
                nc.sync.dma_start(out=vacuity_rows, in_=vacuity[:])
            if 1 <= b < BLOCKS and i < JOINT:
                scale(b - 1, i + 1)
            if 1 <= b < BLOCKS and SUM_LAG <= i < SUM_LAG + JOINT:
                sum_power(b - 1, i - SUM_LAG + 1)
            if 1 <= b <= BLOCKS - SLOTS and BLOCK - JOINT <= i:
                powers(b + SLOTS - 1, 0, GROUPS, (i - (BLOCK - JOINT) + 1,))
            if 2 <= b <= BLOCKS and i == WEIGH_AT:
                weigh(b - 2)
            if step == BLOCK:
                nc.vector.tensor_scalar(out=rank_sum[:], in0=total[:], scalar1=-m_bias * m_bias * pairs, scalar2=None, op0=ALU.add)
        weigh(BLOCKS - 1)
        for side, members in enumerate(bank_stages):
            cols = slice(members[0] * 2 * GT, (members[-1] + 1) * 2 * GT)
            nc.vector.tensor_reduce(
                out=ratio_sum[:, cols].rearrange("p (g t) -> p g t", t=GT), in_=back[side][:].rearrange("p j (i c t) -> p (j i) t c", i=2, t=GT),
                axis=mybir.AxisListType.X, op=ALU.add)
        nc.vector.tensor_tensor(out=dissonance[:], in0=ratio_sum[:], in1=rank_sum[:], op=ALU.add)
        nc.sync.dma_start(out=dissonance_rows, in_=dissonance[:])
